import numpy as np
import ml_dtypes


def mxq(x, axis, fmt="e4m3"):
    dtype, down = {"e4m3": (ml_dtypes.float8_e4m3fn, 7), "e5m2": (ml_dtypes.float8_e5m2, 14)}[fmt]
    v = np.moveaxis(np.asarray(x, np.float32).astype(ml_dtypes.bfloat16).astype(np.float64), axis, -1)
    blocks = v.reshape(v.shape[:-1] + (-1, 32))
    amax = np.abs(blocks).max(-1, keepdims=True)
    byte = np.maximum(np.where(amax > 0, np.frexp(amax)[1] - 1 + 127, 0) - down, 1)
    scale = np.exp2(byte - 127.0)
    codes = (blocks / scale).astype(np.float32).astype(dtype).astype(np.float64)
    return np.moveaxis((codes * scale).reshape(v.shape), -1, axis)


WIDE = False


def mx_kscale(k):
    if not WIDE:
        return np.ones(k)
    levels = np.array([10, -10, 5, -5, 0])
    a = np.random.permutation(np.resize(levels, k // 512 * 4)).reshape(k // 512, 4)
    idx = np.arange(k)
    return np.exp2(a[idx // 512, idx % 128 // 32])


BF16 = ml_dtypes.bfloat16


def bf(x):
    return np.asarray(x, np.float32).astype(BF16)


def f64(x):
    return np.asarray(x).astype(np.float64)


B, T, H, A = 256, 5, 512, 512


def softmax_t(z):
    e = np.exp(z - z.max(axis=1, keepdims=True))
    return e / e.sum(axis=1, keepdims=True)


def setup_inputs():
    s = mx_kscale(2 * H)
    return {"ht": bf(np.random.standard_normal((B, H)) * s[:H]),
            "ct": bf(np.random.standard_normal((B, H)) * s[H:]),
            "hi": bf(np.random.standard_normal((B, T, H))),
            "W_as": bf(np.random.standard_normal((2 * H, A)) * 0.7 / np.sqrt(2 * H) / s[:, None]),
            "W_ah": bf(np.random.standard_normal((H, A)) * 0.7 / np.sqrt(H)),
            "ba": bf(np.random.standard_normal((1, A)) * 0.3),
            "v": bf(np.random.standard_normal((1, A)) * 0.5),
            "W_a": bf(np.random.standard_normal((A, H)) * 2.0 / np.sqrt(A))}


def reference(ht, ct, hi, W_as, W_ah, ba, v, W_a):
    hi = f64(hi)
    q = np.concatenate((f64(ht), f64(ct)), axis=-1)
    a_s = mxq(q, 1, "e4m3") @ mxq(f64(W_as), 0, "e4m3")
    ah = mxq(hi, 2, "e4m3") @ mxq(f64(W_ah), 0, "e4m3")
    etk = np.tanh(a_s[:, None, :] + ah + f64(ba))
    etk = mxq(etk, 2, "e4m3") @ mxq(f64(W_a), 0, "e4m3")
    atk = softmax_t(etk)
    return np.sum(atk * hi, axis=1)

@@ -1,0 +1,279 @@
+from contextlib import ExitStack
+
+import concourse.mybir as mybir
+from concourse.masks import make_identity
+
+FLOPS = 2 * (256 * 1024 * 512 + 2 * 1280 * 512 * 512)
+
+FP8X4 = mybir.dt.float8_e4m3fn_x4
+BF16 = mybir.dt.bfloat16
+F32 = mybir.dt.float32
+U32 = mybir.dt.uint32
+U8 = mybir.dt.uint8
+AF = mybir.ActivationFunctionType
+ALU = mybir.AluOpType
+
+P = 128
+NBT = 2
+T = 5
+H = 512
+A = 512
+
+PIN = False
+MUL_ON_G = ((0, 1, 2, 3, 4), (0, 1, 2))
+
+
+def tile_haint_attention_kernel(tc, ht, ct, hi, W_as, W_ah, ba, v, W_a, out):
+    nc = tc.nc
+    with ExitStack() as ctx:
+        if PIN:
+            ctx.enter_context(tc.manual_schedule())
+        keep = ctx.enter_context(tc.tile_pool(name="keep", bufs=1))
+        work = ctx.enter_context(tc.tile_pool(name="work", bufs=2))
+        psw = ctx.enter_context(tc.psum_pool(name="psw", bufs=3))
+        psz = ctx.enter_context(tc.psum_pool(name="psz", bufs=5))
+
+        ident_f = keep.tile([P, P], F32)
+        make_identity(nc, ident_f[:])
+        ident_b = keep.tile([P, P], BF16)
+        make_identity(nc, ident_b[:])
+        ba16 = keep.tile([P, P], BF16)
+        nc.vector.memset(ba16[:], 0.0)
+
+        wah_raw = keep.tile([P, 4 * A], BF16)
+        was_raw = keep.tile([P, 2 * 4 * A], BF16)
+        wa_raw = keep.tile([P, 4 * H], BF16)
+        q_sb = keep.tile([P, NBT * 2 * H], BF16)
+        hi_sb = keep.tile([P, NBT * T * H], BF16)
+
+        def load_k_pairs(dst, rows):
+            nc.sync.dma_start(
+                out=dst.rearrange("p (u x) -> p u x", u=2),
+                in_=rows.rearrange("(u q e) a -> q u (e a)", u=2, e=2),
+            )
+
+        q_view = q_sb[:].rearrange("p (n s k) -> p n s k", n=NBT, s=2)
+        nc.scalar.dma_start(out=ba16[0:4, :], in_=ba.rearrange("o (j p) -> (o j) p", p=P))
+        load_k_pairs(was_raw[:, 0 : 4 * A], W_as[0:512, :])
+        load_k_pairs(was_raw[:, 4 * A : 8 * A], W_as[512:1024, :])
+        load_k_pairs(wah_raw[:], W_ah)
+        nc.sync.dma_start(out=q_view[:, :, 0, :], in_=ht.rearrange("(n p) k -> p n k", p=P))
+        nc.sync.dma_start(out=q_view[:, :, 1, :], in_=ct.rearrange("(n p) k -> p n k", p=P))
+        nc.sync.dma_start(out=hi_sb[:, 0 : T * H], in_=hi[0:P].rearrange("b t h -> b (t h)"))
+        nc.sync.dma_start(
+            out=hi_sb[:, T * H : 2 * T * H], in_=hi[P : 2 * P].rearrange("b t h -> b (t h)")
+        )
+        nc.sync.dma_start(
+            out=wa_raw[:].rearrange("p (t n) -> p t n", t=4),
+            in_=W_a.rearrange("(t p) n -> p t n", p=P),
+        )
+
+        w_codes = keep.tile([P, 4 * 512], U32, align_bytes=64)
+        w_scales = keep.tile([P, 4 * 512], U8, align_bytes=64)
+        w_grp = keep.tile([P, 4 * 2048], BF16, align_bytes=64)
+        raws = [wah_raw[:], was_raw[:, 0:2048], was_raw[:, 2048:4096], wa_raw[:]]
+
+        def quantise(codes, scales, src):
+            nc.vector.quantize_mx(out=codes.bitcast(FP8X4), scales=scales, in_=src)
+
+        def w_regroup(i):
+            nc.vector.tensor_copy(
+                out=w_grp[:, 2048 * i : 2048 * (i + 1)].rearrange("p (c i t) -> p c t i", i=4, t=4),
+                in_=raws[i].rearrange("p (t c i) -> p c t i", t=4, i=4),
+            )
+
+        def w_quantise(i):
+            quantise(
+                w_codes[:, 512 * i : 512 * (i + 1)],
+                w_scales[:, 512 * i : 512 * (i + 1)],
+                w_grp[:, 2048 * i : 2048 * (i + 1)],
+            )
+
+        w_regroup(1)
+        w_regroup(2)
+        w_quantise(1)
+        w_regroup(0)
+        w_quantise(2)
+        w_quantise(0)
+
+        pb = psw.tile([P, P], BF16, tag="w")
+        nc.tensor.transpose(pb[:], ba16[:], ident_b[:])
+        ba_sb = keep.tile([P, 4], F32)
+        nc.vector.tensor_copy(out=ba_sb[:], in_=pb[:, 0:4])
+
+        q32 = q_sb[:].bitcast(F32)
+        hi32 = hi_sb[:].bitcast(F32)
+        q_codes = keep.tile([P, NBT * 2 * P], U32, align_bytes=64)
+        q_scales = keep.tile([P, NBT * 2 * P], U8, align_bytes=64)
+        hi_codes = keep.tile([P, NBT * T * P], U32, align_bytes=64)
+        hi_scales = keep.tile([P, NBT * T * P], U8, align_bytes=64)
+        q_grp = keep.tile([P, NBT * 2 * P * 4], BF16, align_bytes=64)
+        hi_grp = keep.tile([P, NBT * T * P * 4], BF16, align_bytes=64)
+        q_grp32 = q_grp[:].bitcast(F32)
+        hi_grp32 = hi_grp[:].bitcast(F32)
+
+        def transpose_words(src32, dst32, first, count):
+            xt = psw.tile([P, 4, P], F32, tag="w")
+            for i in range(2 * count):
+                nc.tensor.transpose(
+                    xt[:, i, :], src32[:, 256 * first + P * i : 256 * first + P * (i + 1)], ident_f[:]
+                )
+            nc.scalar.copy(
+                out=dst32[:, 256 * first : 256 * (first + count)].rearrange(
+                    "p (g b u) -> p g b u", g=count, u=2
+                ),
+                in_=xt[:, 0 : 2 * count, :].rearrange("p (g u) b -> p g b u", u=2),
+            )
+
+        transpose_words(q32, q_grp32, 0, 2)
+        transpose_words(q32, q_grp32, 2, 2)
+        quantise(q_codes[:], q_scales[:], q_grp[:])
+        for bt in range(NBT):
+            transpose_words(hi32, hi_grp32, T * bt, 2)
+            transpose_words(hi32, hi_grp32, T * bt + 2, 2)
+            transpose_words(hi32, hi_grp32, T * bt + 4, 1)
+            c0 = T * P * bt
+            quantise(
+                hi_codes[:, c0 : c0 + 512], hi_scales[:, c0 : c0 + 512],
+                hi_grp[:, 4 * c0 : 4 * c0 + 2048],
+            )
+            quantise(
+                hi_codes[:, c0 + 512 : c0 + 640], hi_scales[:, c0 + 512 : c0 + 640],
+                hi_grp[:, 4 * c0 + 2048 : 4 * c0 + 2560],
+            )
+        w_regroup(3)
+        w_quantise(3)
+
+        g_codes = keep.tile([P, NBT * T * P], U32, align_bytes=64)
+        g_scales = keep.tile([P, NBT * T * P], U8, align_bytes=64)
+
+        def mx(out_ap, l_codes, l_scales, lc, r_codes, r_scales, rc, n, start, stop):
+            nc.tensor.matmul_mx(
+                out=out_ap,
+                lhsT=l_codes[:, lc : lc + P].bitcast(FP8X4),
+                lhsT_scale=l_scales[:, lc : lc + P],
+                rhs=r_codes[:, rc : rc + n].bitcast(FP8X4),
+                rhs_scale=r_scales[:, rc : rc + n],
+                start=start,
+                stop=stop,
+            )
+
+        def stage1_group(out_ap, bt, j, t):
+            mx(out_ap, w_codes, w_scales, P * j, hi_codes, hi_scales, P * (T * bt + t), P, True, False)
+            mx(out_ap, w_codes, w_scales, 512 + P * j, q_codes, q_scales, P * (2 * bt), P, False, False)
+            mx(out_ap, w_codes, w_scales, 1024 + P * j, q_codes, q_scales, P * (2 * bt + 1), P, False, True)
+
+        def stage1(bt):
+            gt = work.tile([P, 4, T * P], BF16)
+            gg = work.tile([P, T * P * 4], BF16, align_bytes=64)
+            for j in range(4):
+                acc = psw.tile([P, 4, P], F32, tag="w")
+                for t in range(4):
+                    stage1_group(acc[:, t, :], bt, j, t)
+                nc.scalar.activation(
+                    out=gt[:, j, 0:512], in_=acc[:].rearrange("p t b -> p (t b)"),
+                    func=AF.Tanh, bias=ba_sb[:, j : j + 1], scale=1.0,
+                )
+            acc = psw.tile([P, 4, P], F32, tag="w")
+            for j in range(4):
+                stage1_group(acc[:, j, :], bt, j, 4)
+            for j in range(4):
+                nc.scalar.activation(
+                    out=gt[:, j, 512:640], in_=acc[:, j, :],
+                    func=AF.Tanh, bias=ba_sb[:, j : j + 1], scale=1.0,
+                )
+            c0 = T * P * bt
+
+            def g_regroup(lo, n):
+                nc.vector.tensor_copy(
+                    out=gg[:, 4 * lo : 4 * (lo + n)].rearrange("p (c i j) -> p c j i", i=4, j=4),
+                    in_=gt[:, :, lo : lo + n].rearrange("p j (c i) -> p c j i", i=4),
+                )
+
+            def g_quantise(lo, n):
+                quantise(
+                    g_codes[:, c0 + lo : c0 + lo + n], g_scales[:, c0 + lo : c0 + lo + n],
+                    gg[:, 4 * lo : 4 * (lo + n)],
+                )
+
+            g_regroup(0, 256)
+            g_regroup(256, 256)
+            g_quantise(0, 256)
+            g_quantise(256, 256)
+            g_regroup(512, 128)
+            g_quantise(512, 128)
+
+        s2_all = keep.tile([P, NBT, H], F32)
+        r_all = keep.tile([P, NBT, H], F32)
+        n_banks = []
+        ew = []
+
+        def stage2(bt):
+            zs = []
+            for t in range(T):
+                z = psz.tile([P, H], F32, tag="z")
+                mx(z[:], g_codes, g_scales, P * (T * bt + t), w_codes, w_scales, 1536, 512, True, True)
+                zs.append(z)
+            m = work.tile([P, H], F32)
+            nc.scalar.copy(out=m[:], in_=zs[0][:])
+            for t in range(1, T):
+                for lo in (0, 256):
+                    nc.vector.tensor_tensor(
+                        out=m[:, lo : lo + 256], in0=zs[t][:, lo : lo + 256], in1=m[:, lo : lo + 256],
+                        op=ALU.max,
+                    )
+            d = work.tile([P, T, H], F32)
+            e = work.tile([P, T, H], F32)
+            w = work.tile([P, T, H], F32)
+            hi_bt = hi_sb[:, T * H * bt : T * H * (bt + 1)].rearrange("p (t h) -> p t h", t=T)
+            for t in range(T):
+                nc.vector.tensor_tensor(out=d[:, t, :], in0=zs[t][:], in1=m[:], op=ALU.subtract)
+            for t in range(T):
+                nc.scalar.activation(out=e[:, t, :], in_=d[:, t, :], func=AF.Exp)
+            for t in range(T):
+                eng = nc.gpsimd if t in MUL_ON_G[bt] else nc.vector
+                eng.tensor_tensor(out=w[:, t, :], in0=e[:, t, :], in1=hi_bt[:, t, :], op=ALU.mult)
+            ew.append((e, w))
+
+        def sums(bt):
+            pool, tag = ((psw, "w"), (psz, "z"))[bt]
+            e, w = ew[bt]
+            sT = pool.tile([P, 4, P], F32, tag=tag)
+            nT = pool.tile([P, 4, P], F32, tag=tag)
+            for src, dst in ((e, sT), (w, nT)):
+                for t in range(T):
+                    for c in range(4):
+                        nc.tensor.matmul(
+                            out=dst[:, c, :], lhsT=src[:, t, P * c : P * (c + 1)], rhs=ident_f[:],
+                            is_transpose=True,
+                            start=(t == 0 and c == 0), stop=(t == T - 1 and c == 3),
+                        )
+            nc.scalar.activation(
+                out=s2_all[:, bt, :], in_=sT[:].rearrange("p c b -> p (c b)"), func=AF.Square
+            )
+            n_banks.append(nT)
+
+        stage1(0)
+        stage2(0)
+        stage1(1)
+        sums(0)
+        stage2(1)
+        sums(1)
+
+        nc.scalar.activation(out=r_all[:], in_=s2_all[:], func=AF.Abs_reciprocal_sqrt)
+        for bt in range(NBT):
+            pool, tag = ((psw, "w"), (psz, "z"))[bt]
+            oT = work.tile([P, 4, P], F32)
+            nc.vector.tensor_tensor(
+                out=oT[:].rearrange("p c b -> p (c b)"),
+                in0=n_banks[bt][:].rearrange("p c b -> p (c b)"), in1=r_all[:, bt, :], op=ALU.mult,
+            )
+            o_ps = pool.tile([P, 4, P], F32, tag=tag)
+            for c in range(4):
+                nc.tensor.transpose(o_ps[:, c, :], oT[:, c, :], ident_f[:])
+            o_sb = work.tile([P, H], F32)
+            if bt == 0:
+                nc.scalar.copy(out=o_sb[:], in_=o_ps[:].rearrange("p c h -> p (c h)"))
+            else:
+                nc.vector.tensor_copy(out=o_sb[:], in_=o_ps[:].rearrange("p c h -> p (c h)"))
+            nc.sync.dma_start(out=out[P * bt : P * (bt + 1), :], in_=o_sb[:])

@@ -19,8 +19,10 @@ T = 5
 H = 512
 A = 512
 
-PIN = False
+PIN = True
+V_COLS = 352
 MUL_ON_G = ((0, 1, 2, 3, 4), (0, 1, 2))
+LAG = 2
 
 
 def tile_haint_attention_kernel(tc, ht, ct, hi, W_as, W_ah, ba, v, W_a, out):
@@ -29,7 +31,6 @@ def tile_haint_attention_kernel(tc, ht, ct, hi, W_as, W_ah, ba, v, W_a, out):
         if PIN:
             ctx.enter_context(tc.manual_schedule())
         keep = ctx.enter_context(tc.tile_pool(name="keep", bufs=1))
-        work = ctx.enter_context(tc.tile_pool(name="work", bufs=2))
         psw = ctx.enter_context(tc.psum_pool(name="psw", bufs=3))
         psz = ctx.enter_context(tc.psum_pool(name="psz", bufs=5))
 
@@ -52,21 +53,29 @@ def tile_haint_attention_kernel(tc, ht, ct, hi, W_as, W_ah, ba, v, W_a, out):
                 in_=rows.rearrange("(u q e) a -> q u (e a)", u=2, e=2),
             )
 
-        q_view = q_sb[:].rearrange("p (n s k) -> p n s k", n=NBT, s=2)
+        def load_q(bt):
+            nc.sync.dma_start(out=q_sb[:, 2 * H * bt : 2 * H * bt + H], in_=ht[P * bt : P * (bt + 1), :])
+            nc.sync.dma_start(out=q_sb[:, 2 * H * bt + H : 2 * H * (bt + 1)], in_=ct[P * bt : P * (bt + 1), :])
+
+        def load_hi(bt, t0, t1):
+            nc.sync.dma_start(
+                out=hi_sb[:, H * (T * bt + t0) : H * (T * bt + t1)],
+                in_=hi[P * bt : P * (bt + 1), t0:t1, :].rearrange("b t h -> b (t h)"),
+            )
+
         nc.scalar.dma_start(out=ba16[0:4, :], in_=ba.rearrange("o (j p) -> (o j) p", p=P))
         load_k_pairs(was_raw[:, 0 : 4 * A], W_as[0:512, :])
         load_k_pairs(was_raw[:, 4 * A : 8 * A], W_as[512:1024, :])
         load_k_pairs(wah_raw[:], W_ah)
-        nc.sync.dma_start(out=q_view[:, :, 0, :], in_=ht.rearrange("(n p) k -> p n k", p=P))
-        nc.sync.dma_start(out=q_view[:, :, 1, :], in_=ct.rearrange("(n p) k -> p n k", p=P))
-        nc.sync.dma_start(out=hi_sb[:, 0 : T * H], in_=hi[0:P].rearrange("b t h -> b (t h)"))
-        nc.sync.dma_start(
-            out=hi_sb[:, T * H : 2 * T * H], in_=hi[P : 2 * P].rearrange("b t h -> b (t h)")
-        )
+        load_q(0)
+        load_hi(0, 0, 2)
+        load_hi(0, 2, 5)
         nc.sync.dma_start(
             out=wa_raw[:].rearrange("p (t n) -> p t n", t=4),
             in_=W_a.rearrange("(t p) n -> p t n", p=P),
         )
+        load_q(1)
+        load_hi(1, 0, 5)
 
         w_codes = keep.tile([P, 4 * 512], U32, align_bytes=64)
         w_scales = keep.tile([P, 4 * 512], U8, align_bytes=64)
@@ -76,11 +85,16 @@ def tile_haint_attention_kernel(tc, ht, ct, hi, W_as, W_ah, ba, v, W_a, out):
         def quantise(codes, scales, src):
             nc.vector.quantize_mx(out=codes.bitcast(FP8X4), scales=scales, in_=src)
 
-        def w_regroup(i):
-            nc.vector.tensor_copy(
-                out=w_grp[:, 2048 * i : 2048 * (i + 1)].rearrange("p (c i t) -> p c t i", i=4, t=4),
-                in_=raws[i].rearrange("p (t c i) -> p c t i", t=4, i=4),
-            )
+        def w_regroup(i, v_cols):
+            src = raws[i].rearrange("p (t c) -> p t c", t=4)
+            for copy, lo, hi_c in ((nc.vector.tensor_copy, 0, v_cols), (nc.scalar.copy, v_cols, 512)):
+                if hi_c > lo:
+                    copy(
+                        out=w_grp[:, 2048 * i + 4 * lo : 2048 * i + 4 * hi_c].rearrange(
+                            "p (c i t) -> p c t i", i=4, t=4
+                        ),
+                        in_=src[:, :, lo:hi_c].rearrange("p t (c i) -> p c t i", i=4),
+                    )
 
         def w_quantise(i):
             quantise(
@@ -88,18 +102,6 @@ def tile_haint_attention_kernel(tc, ht, ct, hi, W_as, W_ah, ba, v, W_a, out):
                 w_scales[:, 512 * i : 512 * (i + 1)],
                 w_grp[:, 2048 * i : 2048 * (i + 1)],
             )
-
-        w_regroup(1)
-        w_regroup(2)
-        w_quantise(1)
-        w_regroup(0)
-        w_quantise(2)
-        w_quantise(0)
-
-        pb = psw.tile([P, P], BF16, tag="w")
-        nc.tensor.transpose(pb[:], ba16[:], ident_b[:])
-        ba_sb = keep.tile([P, 4], F32)
-        nc.vector.tensor_copy(out=ba_sb[:], in_=pb[:, 0:4])
 
         q32 = q_sb[:].bitcast(F32)
         hi32 = hi_sb[:].bitcast(F32)
@@ -125,27 +127,30 @@ def tile_haint_attention_kernel(tc, ht, ct, hi, W_as, W_ah, ba, v, W_a, out):
                 in_=xt[:, 0 : 2 * count, :].rearrange("p (g u) b -> p g b u", u=2),
             )
 
-        transpose_words(q32, q_grp32, 0, 2)
-        transpose_words(q32, q_grp32, 2, 2)
-        quantise(q_codes[:], q_scales[:], q_grp[:])
-        for bt in range(NBT):
-            transpose_words(hi32, hi_grp32, T * bt, 2)
-            transpose_words(hi32, hi_grp32, T * bt + 2, 2)
-            transpose_words(hi32, hi_grp32, T * bt + 4, 1)
-            c0 = T * P * bt
+        def q_rows(bt):
+            transpose_words(q32, q_grp32, 2 * bt, 2)
+
+        def q_quantise(bt):
             quantise(
-                hi_codes[:, c0 : c0 + 512], hi_scales[:, c0 : c0 + 512],
-                hi_grp[:, 4 * c0 : 4 * c0 + 2048],
+                q_codes[:, 256 * bt : 256 * (bt + 1)], q_scales[:, 256 * bt : 256 * (bt + 1)],
+                q_grp[:, 1024 * bt : 1024 * (bt + 1)],
             )
+
+        def hi_rows(bt, t0, count):
+            transpose_words(hi32, hi_grp32, T * bt + t0, count)
+
+        def hi_quantise(bt, t0, count):
+            c0 = P * (T * bt + t0)
             quantise(
-                hi_codes[:, c0 + 512 : c0 + 640], hi_scales[:, c0 + 512 : c0 + 640],
-                hi_grp[:, 4 * c0 + 2048 : 4 * c0 + 2560],
+                hi_codes[:, c0 : c0 + P * count], hi_scales[:, c0 : c0 + P * count],
+                hi_grp[:, 4 * c0 : 4 * (c0 + P * count)],
             )
-        w_regroup(3)
-        w_quantise(3)
 
         g_codes = keep.tile([P, NBT * T * P], U32, align_bytes=64)
         g_scales = keep.tile([P, NBT * T * P], U8, align_bytes=64)
+        gt = keep.tile([P, NBT * T, 4, P], BF16)
+        gg = keep.tile([P, NBT * T * P * 4], BF16, align_bytes=64)
+        ba_sb = keep.tile([P, 4], F32)
 
         def mx(out_ap, l_codes, l_scales, lc, r_codes, r_scales, rc, n, start, stop):
             nc.tensor.matmul_mx(
@@ -158,122 +163,187 @@ def tile_haint_attention_kernel(tc, ht, ct, hi, W_as, W_ah, ba, v, W_a, out):
                 stop=stop,
             )
 
-        def stage1_group(out_ap, bt, j, t):
-            mx(out_ap, w_codes, w_scales, P * j, hi_codes, hi_scales, P * (T * bt + t), P, True, False)
-            mx(out_ap, w_codes, w_scales, 512 + P * j, q_codes, q_scales, P * (2 * bt), P, False, False)
-            mx(out_ap, w_codes, w_scales, 1024 + P * j, q_codes, q_scales, P * (2 * bt + 1), P, False, True)
-
-        def stage1(bt):
-            gt = work.tile([P, 4, T * P], BF16)
-            gg = work.tile([P, T * P * 4], BF16, align_bytes=64)
-            for j in range(4):
-                acc = psw.tile([P, 4, P], F32, tag="w")
-                for t in range(4):
-                    stage1_group(acc[:, t, :], bt, j, t)
-                nc.scalar.activation(
-                    out=gt[:, j, 0:512], in_=acc[:].rearrange("p t b -> p (t b)"),
-                    func=AF.Tanh, bias=ba_sb[:, j : j + 1], scale=1.0,
-                )
+        def stage1(bt, t):
             acc = psw.tile([P, 4, P], F32, tag="w")
             for j in range(4):
-                stage1_group(acc[:, j, :], bt, j, 4)
+                o = acc[:, j, :]
+                mx(o, w_codes, w_scales, P * j, hi_codes, hi_scales, P * (T * bt + t), P, True, False)
+                mx(o, w_codes, w_scales, 512 + P * j, q_codes, q_scales, P * (2 * bt), P, False, False)
+                mx(o, w_codes, w_scales, 1024 + P * j, q_codes, q_scales, P * (2 * bt + 1), P, False, True)
             for j in range(4):
                 nc.scalar.activation(
-                    out=gt[:, j, 512:640], in_=acc[:, j, :],
+                    out=gt[:, T * bt + t, j, :], in_=acc[:, j, :],
                     func=AF.Tanh, bias=ba_sb[:, j : j + 1], scale=1.0,
                 )
-            c0 = T * P * bt
 
-            def g_regroup(lo, n):
-                nc.vector.tensor_copy(
-                    out=gg[:, 4 * lo : 4 * (lo + n)].rearrange("p (c i j) -> p c j i", i=4, j=4),
-                    in_=gt[:, :, lo : lo + n].rearrange("p j (c i) -> p c j i", i=4),
-                )
-
-            def g_quantise(lo, n):
-                quantise(
-                    g_codes[:, c0 + lo : c0 + lo + n], g_scales[:, c0 + lo : c0 + lo + n],
-                    gg[:, 4 * lo : 4 * (lo + n)],
-                )
-
-            g_regroup(0, 256)
-            g_regroup(256, 256)
-            g_quantise(0, 256)
-            g_quantise(256, 256)
-            g_regroup(512, 128)
-            g_quantise(512, 128)
-
-        s2_all = keep.tile([P, NBT, H], F32)
-        r_all = keep.tile([P, NBT, H], F32)
-        n_banks = []
-        ew = []
-
-        def stage2(bt):
-            zs = []
-            for t in range(T):
-                z = psz.tile([P, H], F32, tag="z")
-                mx(z[:], g_codes, g_scales, P * (T * bt + t), w_codes, w_scales, 1536, 512, True, True)
-                zs.append(z)
-            m = work.tile([P, H], F32)
-            nc.scalar.copy(out=m[:], in_=zs[0][:])
-            for t in range(1, T):
-                for lo in (0, 256):
-                    nc.vector.tensor_tensor(
-                        out=m[:, lo : lo + 256], in0=zs[t][:, lo : lo + 256], in1=m[:, lo : lo + 256],
-                        op=ALU.max,
-                    )
-            d = work.tile([P, T, H], F32)
-            e = work.tile([P, T, H], F32)
-            w = work.tile([P, T, H], F32)
-            hi_bt = hi_sb[:, T * H * bt : T * H * (bt + 1)].rearrange("p (t h) -> p t h", t=T)
-            for t in range(T):
-                nc.vector.tensor_tensor(out=d[:, t, :], in0=zs[t][:], in1=m[:], op=ALU.subtract)
-            for t in range(T):
-                nc.scalar.activation(out=e[:, t, :], in_=d[:, t, :], func=AF.Exp)
-            for t in range(T):
-                eng = nc.gpsimd if t in MUL_ON_G[bt] else nc.vector
-                eng.tensor_tensor(out=w[:, t, :], in0=e[:, t, :], in1=hi_bt[:, t, :], op=ALU.mult)
-            ew.append((e, w))
-
-        def sums(bt):
-            pool, tag = ((psw, "w"), (psz, "z"))[bt]
-            e, w = ew[bt]
-            sT = pool.tile([P, 4, P], F32, tag=tag)
-            nT = pool.tile([P, 4, P], F32, tag=tag)
-            for src, dst in ((e, sT), (w, nT)):
-                for t in range(T):
-                    for c in range(4):
-                        nc.tensor.matmul(
-                            out=dst[:, c, :], lhsT=src[:, t, P * c : P * (c + 1)], rhs=ident_f[:],
-                            is_transpose=True,
-                            start=(t == 0 and c == 0), stop=(t == T - 1 and c == 3),
-                        )
-            nc.scalar.activation(
-                out=s2_all[:, bt, :], in_=sT[:].rearrange("p c b -> p (c b)"), func=AF.Square
+        def g_regroup(bt, t):
+            k = T * bt + t
+            nc.vector.tensor_copy(
+                out=gg[:, 512 * k : 512 * (k + 1)].rearrange("p (c i j) -> p c j i", i=4, j=4),
+                in_=gt[:, k, :, :].rearrange("p j (c i) -> p c j i", i=4),
             )
-            n_banks.append(nT)
 
-        stage1(0)
-        stage2(0)
-        stage1(1)
-        sums(0)
-        stage2(1)
-        sums(1)
+        def g_quantise(bt, t):
+            k = T * bt + t
+            quantise(
+                g_codes[:, P * k : P * (k + 1)], g_scales[:, P * k : P * (k + 1)],
+                gg[:, 512 * k : 512 * (k + 1)],
+            )
 
-        nc.scalar.activation(out=r_all[:], in_=s2_all[:], func=AF.Abs_reciprocal_sqrt)
-        for bt in range(NBT):
-            pool, tag = ((psw, "w"), (psz, "z"))[bt]
-            oT = work.tile([P, 4, P], F32)
+        m = keep.tile([P, NBT, H], F32)
+        d = keep.tile([P, NBT * T, H], F32)
+        e = keep.tile([P, NBT * T, H], F32)
+        w = keep.tile([P, NBT * T, H], F32)
+        s2 = keep.tile([P, NBT, H], F32)
+        r = keep.tile([P, NBT, H], F32)
+        oT = keep.tile([P, NBT, 4, P], F32)
+        o_sb = keep.tile([P, NBT, H], F32)
+        zs = {}
+        sums = {}
+
+        def stage2(bt, t):
+            z = psz.tile([P, H], F32, tag="z")
+            mx(z[:], g_codes, g_scales, P * (T * bt + t), w_codes, w_scales, 1536, 512, True, True)
+            zs[(bt, t)] = z
+            if t == 0:
+                nc.scalar.copy(out=m[:, bt, :], in_=z[:])
+            else:
+                nc.vector.tensor_tensor(out=m[:, bt, :], in0=z[:], in1=m[:, bt, :], op=ALU.max)
+
+        def subtract(bt, t):
             nc.vector.tensor_tensor(
-                out=oT[:].rearrange("p c b -> p (c b)"),
-                in0=n_banks[bt][:].rearrange("p c b -> p (c b)"), in1=r_all[:, bt, :], op=ALU.mult,
+                out=d[:, T * bt + t, :], in0=zs[(bt, t)][:], in1=m[:, bt, :], op=ALU.subtract
             )
+
+        def exponent(bt, t):
+            nc.scalar.activation(out=e[:, T * bt + t, :], in_=d[:, T * bt + t, :], func=AF.Exp)
+
+        def product(bt, t):
+            k = T * bt + t
+            eng = nc.gpsimd if t in MUL_ON_G[bt] else nc.vector
+            eng.tensor_tensor(
+                out=w[:, k, :], in0=e[:, k, :], in1=hi_sb[:, H * k : H * (k + 1)], op=ALU.mult
+            )
+
+        def open_sum(bt, what):
+            pool, tag = ((psw, "w"), (psz, "z"))[bt]
+            acc_t = pool.tile([P, 4, P], F32, tag=tag)
+            sums[(bt, what)] = acc_t
+
+        def add_to_sum(bt, what, t):
+            src = (e, w)[what]
+            for c in range(4):
+                nc.tensor.matmul(
+                    out=sums[(bt, what)][:, c, :], lhsT=src[:, T * bt + t, P * c : P * (c + 1)],
+                    rhs=ident_f[:], is_transpose=True,
+                    start=(t == 0 and c == 0), stop=(t == T - 1 and c == 3),
+                )
+
+        def square_sum(bt):
+            nc.scalar.activation(
+                out=s2[:, bt, :], in_=sums[(bt, 0)][:].rearrange("p c b -> p (c b)"), func=AF.Square
+            )
+
+        def one_over(bt):
+            nc.scalar.activation(out=r[:, bt, :], in_=s2[:, bt, :], func=AF.Abs_reciprocal_sqrt)
+
+        def normalise(bt):
+            nc.vector.tensor_tensor(
+                out=oT[:, bt, :, :].rearrange("p c b -> p (c b)"),
+                in0=sums[(bt, 1)][:].rearrange("p c b -> p (c b)"), in1=r[:, bt, :], op=ALU.mult,
+            )
+
+        def store(bt):
+            pool, tag = ((psw, "w"), (psz, "z"))[bt]
             o_ps = pool.tile([P, 4, P], F32, tag=tag)
             for c in range(4):
-                nc.tensor.transpose(o_ps[:, c, :], oT[:, c, :], ident_f[:])
-            o_sb = work.tile([P, H], F32)
-            if bt == 0:
-                nc.scalar.copy(out=o_sb[:], in_=o_ps[:].rearrange("p c h -> p (c h)"))
-            else:
-                nc.vector.tensor_copy(out=o_sb[:], in_=o_ps[:].rearrange("p c h -> p (c h)"))
-            nc.sync.dma_start(out=out[P * bt : P * (bt + 1), :], in_=o_sb[:])
+                nc.tensor.transpose(o_ps[:, c, :], oT[:, bt, c, :], ident_f[:])
+            copy = (nc.scalar.copy, nc.vector.tensor_copy)[bt]
+            copy(out=o_sb[:, bt, :], in_=o_ps[:].rearrange("p c h -> p (c h)"))
+            nc.sync.dma_start(out=out[P * bt : P * (bt + 1), :], in_=o_sb[:, bt, :])
+
+        w_regroup(1, V_COLS)
+        w_regroup(2, V_COLS)
+        w_quantise(1)
+        w_regroup(0, V_COLS)
+        w_quantise(2)
+        w_quantise(0)
+        pb = psw.tile([P, P], BF16, tag="w")
+        nc.tensor.transpose(pb[:], ba16[:], ident_b[:])
+        nc.vector.tensor_copy(out=ba_sb[:], in_=pb[:, 0:4])
+        q_rows(0)
+        hi_rows(0, 0, 2)
+        q_quantise(0)
+        hi_quantise(0, 0, 2)
+        hi_rows(0, 2, 2)
+        hi_rows(0, 4, 1)
+        hi_quantise(0, 2, 2)
+        w_regroup(3, 512)
+        hi_quantise(0, 4, 1)
+        w_quantise(3)
+
+        for t in range(T + LAG):
+            if t < T:
+                stage1(0, t)
+                g_regroup(0, t)
+            if t == T:
+                q_rows(1)
+                hi_rows(1, 0, 2)
+            if t == T + 1:
+                hi_rows(1, 2, 2)
+                hi_rows(1, 4, 1)
+            if t >= LAG:
+                stage2(0, t - LAG)
+            if t < T:
+                g_quantise(0, t)
+            if t == T:
+                q_quantise(1)
+                hi_quantise(1, 0, 2)
+            if t == T + 1:
+                hi_quantise(1, 2, 2)
+                hi_quantise(1, 4, 1)
+
+        for t in range(T + LAG):
+            if t < T:
+                subtract(0, t)
+            if 1 <= t <= T:
+                exponent(0, t - 1)
+                product(0, t - 1)
+            if t < T:
+                stage1(1, t)
+                g_regroup(1, t)
+            if t == T:
+                open_sum(0, 0)
+                add_to_sum(0, 0, 0)
+                add_to_sum(0, 0, 1)
+            if t == T + 1:
+                add_to_sum(0, 0, 2)
+                add_to_sum(0, 0, 3)
+                add_to_sum(0, 0, 4)
+                square_sum(0)
+            if t >= LAG:
+                stage2(1, t - LAG)
+            if t < T:
+                g_quantise(1, t)
+        open_sum(0, 1)
+        for t in range(T):
+            add_to_sum(0, 1, t)
+
+        open_sum(1, 0)
+        open_sum(1, 1)
+        for t in range(T):
+            subtract(1, t)
+        for t in range(T):
+            exponent(1, t)
+            product(1, t)
+            add_to_sum(1, 0, t)
+            if t >= 1:
+                add_to_sum(1, 1, t - 1)
+        add_to_sum(1, 1, T - 1)
+        one_over(0)
+        square_sum(1)
+        one_over(1)
+        normalise(0)
+        store(0)
+        normalise(1)
+        store(1)

@@ -21,8 +21,8 @@ A = 512
 
 PIN = True
 V_COLS = 352
-MUL_ON_G = ((0, 1, 2, 3, 4), (0, 1, 2))
-LAG = 2
+MUL_ON_G = ((0, 1, 2, 3, 4), ())
+UNITS = ((0, 2), (2, 2), (4, 1))
 
 
 def tile_haint_attention_kernel(tc, ht, ct, hi, W_as, W_ah, ba, v, W_a, out):
@@ -148,7 +148,7 @@ def tile_haint_attention_kernel(tc, ht, ct, hi, W_as, W_ah, ba, v, W_a, out):
 
         g_codes = keep.tile([P, NBT * T * P], U32, align_bytes=64)
         g_scales = keep.tile([P, NBT * T * P], U8, align_bytes=64)
-        gt = keep.tile([P, NBT * T, 4, P], BF16)
+        gt = keep.tile([P, 4, NBT * T * P], BF16)
         gg = keep.tile([P, NBT * T * P * 4], BF16, align_bytes=64)
         ba_sb = keep.tile([P, 4], F32)
 
@@ -163,31 +163,37 @@ def tile_haint_attention_kernel(tc, ht, ct, hi, W_as, W_ah, ba, v, W_a, out):
                 stop=stop,
             )
 
-        def stage1(bt, t):
-            acc = psw.tile([P, 4, P], F32, tag="w")
-            for j in range(4):
-                o = acc[:, j, :]
-                mx(o, w_codes, w_scales, P * j, hi_codes, hi_scales, P * (T * bt + t), P, True, False)
-                mx(o, w_codes, w_scales, 512 + P * j, q_codes, q_scales, P * (2 * bt), P, False, False)
-                mx(o, w_codes, w_scales, 1024 + P * j, q_codes, q_scales, P * (2 * bt + 1), P, False, True)
-            for j in range(4):
-                nc.scalar.activation(
-                    out=gt[:, T * bt + t, j, :], in_=acc[:, j, :],
-                    func=AF.Tanh, bias=ba_sb[:, j : j + 1], scale=1.0,
-                )
+        def stage1_group(o, bt, j, t):
+            mx(o, w_codes, w_scales, P * j, hi_codes, hi_scales, P * (T * bt + t), P, True, False)
+            mx(o, w_codes, w_scales, 512 + P * j, q_codes, q_scales, P * (2 * bt), P, False, False)
+            mx(o, w_codes, w_scales, 1024 + P * j, q_codes, q_scales, P * (2 * bt + 1), P, False, True)
 
-        def g_regroup(bt, t):
-            k = T * bt + t
+        def stage1(bt, t0, count):
+            c0 = P * (T * bt + t0)
+            j_per_bank = 4 // count
+            for j0 in range(0, 4, j_per_bank):
+                acc = psw.tile([P, j_per_bank, count * P], F32, tag="w")
+                for jj in range(j_per_bank):
+                    for tt in range(count):
+                        stage1_group(acc[:, jj, P * tt : P * (tt + 1)], bt, j0 + jj, t0 + tt)
+                for jj in range(j_per_bank):
+                    nc.scalar.activation(
+                        out=gt[:, j0 + jj, c0 : c0 + P * count], in_=acc[:, jj, :],
+                        func=AF.Tanh, bias=ba_sb[:, j0 + jj : j0 + jj + 1], scale=1.0,
+                    )
+
+        def g_regroup(bt, t0, count):
+            c0 = P * (T * bt + t0)
             nc.vector.tensor_copy(
-                out=gg[:, 512 * k : 512 * (k + 1)].rearrange("p (c i j) -> p c j i", i=4, j=4),
-                in_=gt[:, k, :, :].rearrange("p j (c i) -> p c j i", i=4),
+                out=gg[:, 4 * c0 : 4 * (c0 + P * count)].rearrange("p (c i j) -> p c j i", i=4, j=4),
+                in_=gt[:, :, c0 : c0 + P * count].rearrange("p j (c i) -> p c j i", i=4),
             )
 
-        def g_quantise(bt, t):
-            k = T * bt + t
+        def g_quantise(bt, t0, count):
+            c0 = P * (T * bt + t0)
             quantise(
-                g_codes[:, P * k : P * (k + 1)], g_scales[:, P * k : P * (k + 1)],
-                gg[:, 512 * k : 512 * (k + 1)],
+                g_codes[:, c0 : c0 + P * count], g_scales[:, c0 : c0 + P * count],
+                gg[:, 4 * c0 : 4 * (c0 + P * count)],
             )
 
         m = keep.tile([P, NBT, H], F32)
@@ -277,69 +283,60 @@ def tile_haint_attention_kernel(tc, ht, ct, hi, W_as, W_ah, ba, v, W_a, out):
         hi_quantise(0, 0, 2)
         hi_rows(0, 2, 2)
         hi_rows(0, 4, 1)
-        hi_quantise(0, 2, 2)
         w_regroup(3, 512)
-        hi_quantise(0, 4, 1)
+        hi_quantise(0, 2, 2)
         w_quantise(3)
+        hi_quantise(0, 4, 1)
 
-        for t in range(T + LAG):
-            if t < T:
-                stage1(0, t)
-                g_regroup(0, t)
-            if t == T:
-                q_rows(1)
-                hi_rows(1, 0, 2)
-            if t == T + 1:
-                hi_rows(1, 2, 2)
-                hi_rows(1, 4, 1)
-            if t >= LAG:
-                stage2(0, t - LAG)
-            if t < T:
-                g_quantise(0, t)
-            if t == T:
-                q_quantise(1)
-                hi_quantise(1, 0, 2)
-            if t == T + 1:
-                hi_quantise(1, 2, 2)
-                hi_quantise(1, 4, 1)
+        for t0, count in UNITS:
+            stage1(0, t0, count)
+            g_regroup(0, t0, count)
+            g_quantise(0, t0, count)
 
-        for t in range(T + LAG):
-            if t < T:
-                subtract(0, t)
-            if 1 <= t <= T:
-                exponent(0, t - 1)
-                product(0, t - 1)
-            if t < T:
-                stage1(1, t)
-                g_regroup(1, t)
-            if t == T:
-                open_sum(0, 0)
-                add_to_sum(0, 0, 0)
-                add_to_sum(0, 0, 1)
-            if t == T + 1:
-                add_to_sum(0, 0, 2)
-                add_to_sum(0, 0, 3)
-                add_to_sum(0, 0, 4)
-                square_sum(0)
-            if t >= LAG:
-                stage2(1, t - LAG)
-            if t < T:
-                g_quantise(1, t)
+        q_rows(1)
+        hi_rows(1, 0, 2)
+        q_quantise(1)
+        hi_quantise(1, 0, 2)
+        for t in range(3):
+            stage2(0, t)
+        hi_rows(1, 2, 2)
+        hi_rows(1, 4, 1)
+        hi_quantise(1, 2, 2)
+        hi_quantise(1, 4, 1)
+        for t in range(3, T):
+            stage2(0, t)
+
+        for u in range(3):
+            t0, count = UNITS[u]
+            stage1(1, t0, count)
+            g_regroup(1, t0, count)
+            subtract(0, 2 * u)
+            g_quantise(1, t0, count)
+            if 2 * u + 1 < T:
+                subtract(0, 2 * u + 1)
+        for t in range(T):
+            stage2(1, t)
+
+        open_sum(0, 0)
+        for t in range(T):
+            exponent(0, t)
+            product(0, t)
+            add_to_sum(0, 0, t)
+        square_sum(0)
         open_sum(0, 1)
         for t in range(T):
             add_to_sum(0, 1, t)
 
-        open_sum(1, 0)
-        open_sum(1, 1)
         for t in range(T):
             subtract(1, t)
+        open_sum(1, 0)
         for t in range(T):
             exponent(1, t)
-            product(1, t)
             add_to_sum(1, 0, t)
-            if t >= 1:
-                add_to_sum(1, 1, t - 1)
-        add_to_sum(1, 1, T - 1)
+        open_sum(1, 1)
+        for t in range(T):
+            product(1, t)
+            add_to_sum(1, 1, t)
         one_over(0)
         square_sum(1)
         one_over(1)

@@ -231,12 +231,22 @@ def tile_haint_attention_kernel(tc, ht, ct, hi, W_as, W_ah, ba, v, W_a, out):
                 out=w[:, k, :], in0=e[:, k, :], in1=hi_sb[:, H * k : H * (k + 1)], op=ALU.mult
             )
 
+        warm = {"n": 0, "tile": None}
+
+        def keep_warm(transposes, every):
+            warm["n"] = warm["n"] + transposes
+            if warm["n"] >= every:
+                warm["n"] = 0
+                nc.tensor.matmul(
+                    out=warm["tile"][:, 0:256], lhsT=ident_f[:], rhs=m[:, 0, 0:256], start=True, stop=True
+                )
+
         def open_sum(bt, what):
             pool, tag = ((psw, "w"), (psz, "z"))[bt]
             acc_t = pool.tile([P, 4, P], F32, tag=tag)
             sums[(bt, what)] = acc_t
 
-        def add_to_sum(bt, what, t):
+        def add_to_sum(bt, what, t, every):
             src = (e, w)[what]
             for c in range(4):
                 nc.tensor.matmul(
@@ -244,6 +254,7 @@ def tile_haint_attention_kernel(tc, ht, ct, hi, W_as, W_ah, ba, v, W_a, out):
                     rhs=ident_f[:], is_transpose=True,
                     start=(t == 0 and c == 0), stop=(t == T - 1 and c == 3),
                 )
+            keep_warm(4, every)
 
         def square_sum(bt):
             nc.scalar.activation(
@@ -318,25 +329,27 @@ def tile_haint_attention_kernel(tc, ht, ct, hi, W_as, W_ah, ba, v, W_a, out):
             stage2(1, t)
 
         open_sum(0, 0)
+        open_sum(0, 1)
+        idle_bank = psw.tile([P, H], F32, tag="w")
+        warm["tile"] = idle_bank
         for t in range(T):
             exponent(0, t)
             product(0, t)
-            add_to_sum(0, 0, t)
+            add_to_sum(0, 0, t, 8)
         square_sum(0)
-        open_sum(0, 1)
         for t in range(T):
-            add_to_sum(0, 1, t)
+            add_to_sum(0, 1, t, 4)
 
         for t in range(T):
             subtract(1, t)
         open_sum(1, 0)
         for t in range(T):
             exponent(1, t)
-            add_to_sum(1, 0, t)
+            add_to_sum(1, 0, t, 8)
         open_sum(1, 1)
         for t in range(T):
             product(1, t)
-            add_to_sum(1, 1, t)
+            add_to_sum(1, 1, t, 8)
         one_over(0)
         square_sum(1)
         one_over(1)

@@ -21,7 +21,7 @@ A = 512
 
 PIN = True
 V_COLS = 352
-MUL_ON_G = ((0, 1, 2, 3, 4), ())
+MUL_ON_G = ((0, 1, 2, 3, 4), (0, 1))
 UNITS = ((0, 2), (2, 2), (4, 1))
 
 
@@ -204,6 +204,7 @@ def tile_haint_attention_kernel(tc, ht, ct, hi, W_as, W_ah, ba, v, W_a, out):
         r = keep.tile([P, NBT, H], F32)
         oT = keep.tile([P, NBT, 4, P], F32)
         o_sb = keep.tile([P, NBT, H], F32)
+        part = keep.tile([P, 2, H], F32)
         zs = {}
         sums = {}
 
@@ -231,22 +232,12 @@ def tile_haint_attention_kernel(tc, ht, ct, hi, W_as, W_ah, ba, v, W_a, out):
                 out=w[:, k, :], in0=e[:, k, :], in1=hi_sb[:, H * k : H * (k + 1)], op=ALU.mult
             )
 
-        warm = {"n": 0, "tile": None}
-
-        def keep_warm(transposes, every):
-            warm["n"] = warm["n"] + transposes
-            if warm["n"] >= every:
-                warm["n"] = 0
-                nc.tensor.matmul(
-                    out=warm["tile"][:, 0:256], lhsT=ident_f[:], rhs=m[:, 0, 0:256], start=True, stop=True
-                )
-
         def open_sum(bt, what):
             pool, tag = ((psw, "w"), (psz, "z"))[bt]
             acc_t = pool.tile([P, 4, P], F32, tag=tag)
             sums[(bt, what)] = acc_t
 
-        def add_to_sum(bt, what, t, every):
+        def add_to_sum(bt, what, t):
             src = (e, w)[what]
             for c in range(4):
                 nc.tensor.matmul(
@@ -254,7 +245,6 @@ def tile_haint_attention_kernel(tc, ht, ct, hi, W_as, W_ah, ba, v, W_a, out):
                     rhs=ident_f[:], is_transpose=True,
                     start=(t == 0 and c == 0), stop=(t == T - 1 and c == 3),
                 )
-            keep_warm(4, every)
 
         def square_sum(bt):
             nc.scalar.activation(
@@ -325,35 +315,62 @@ def tile_haint_attention_kernel(tc, ht, ct, hi, W_as, W_ah, ba, v, W_a, out):
             g_quantise(1, t0, count)
             if 2 * u + 1 < T:
                 subtract(0, 2 * u + 1)
-        for t in range(T):
-            stage2(1, t)
-
+        stage2(1, 0)
+        stage2(1, 1)
+        exponent(0, 0)
+        product(0, 0)
+        exponent(0, 1)
+        product(0, 1)
         open_sum(0, 0)
-        open_sum(0, 1)
-        idle_bank = psw.tile([P, H], F32, tag="w")
-        warm["tile"] = idle_bank
-        for t in range(T):
-            exponent(0, t)
-            product(0, t)
-            add_to_sum(0, 0, t, 8)
+        add_to_sum(0, 0, 0)
+        stage2(1, 2)
+        exponent(0, 2)
+        product(0, 2)
+        add_to_sum(0, 0, 1)
+        stage2(1, 3)
+        exponent(0, 3)
+        product(0, 3)
+        add_to_sum(0, 0, 2)
+        add_to_sum(0, 0, 3)
+        stage2(1, 4)
+        exponent(0, 4)
+        product(0, 4)
+        add_to_sum(0, 0, 4)
         square_sum(0)
-        for t in range(T):
-            add_to_sum(0, 1, t, 4)
+        open_sum(0, 1)
+        for t in range(3):
+            add_to_sum(0, 1, t)
 
         for t in range(T):
             subtract(1, t)
         open_sum(1, 0)
         for t in range(T):
             exponent(1, t)
-            add_to_sum(1, 0, t, 8)
-        open_sum(1, 1)
-        for t in range(T):
-            product(1, t)
-            add_to_sum(1, 1, t, 8)
+            if t in MUL_ON_G[1]:
+                product(1, t)
+            add_to_sum(1, 0, t)
+            if 1 <= t <= 2:
+                add_to_sum(0, 1, t + 2)
         one_over(0)
         square_sum(1)
         one_over(1)
+
+        def add(dst, a, b):
+            nc.vector.tensor_tensor(out=dst, in0=a, in1=b, op=ALU.add)
+
+        product(1, 2)
+        product(1, 3)
+        add(part[:, 0, :], w[:, T + 2, :], w[:, T + 3, :])
+        product(1, 4)
+        add(part[:, 0, :], part[:, 0, :], w[:, T + 4, :])
+        add(part[:, 1, :], w[:, T, :], w[:, T + 1, :])
         normalise(0)
+        add(part[:, 0, :], part[:, 0, :], part[:, 1, :])
         store(0)
-        normalise(1)
-        store(1)
+        r_ps = psz.tile([P, 4, P], F32, tag="z")
+        for c in range(4):
+            nc.tensor.transpose(r_ps[:, c, :], r[:, 1, P * c : P * (c + 1)], ident_f[:])
+        nc.vector.tensor_tensor(
+            out=o_sb[:, 1, :], in0=r_ps[:].rearrange("p c h -> p (c h)"), in1=part[:, 0, :], op=ALU.mult
+        )
+        nc.sync.dma_start(out=out[P : 2 * P, :], in_=o_sb[:, 1, :])

@@ -21,7 +21,7 @@ A = 512
 
 PIN = True
 V_COLS = 352
-MUL_ON_G = ((0, 1, 2, 3, 4), (0, 1))
+MUL_ON_G = ((0, 1, 2, 3, 4), ())
 UNITS = ((0, 2), (2, 2), (4, 1))
 
 
@@ -204,7 +204,6 @@ def tile_haint_attention_kernel(tc, ht, ct, hi, W_as, W_ah, ba, v, W_a, out):
         r = keep.tile([P, NBT, H], F32)
         oT = keep.tile([P, NBT, 4, P], F32)
         o_sb = keep.tile([P, NBT, H], F32)
-        part = keep.tile([P, 2, H], F32)
         zs = {}
         sums = {}
 
@@ -215,7 +214,11 @@ def tile_haint_attention_kernel(tc, ht, ct, hi, W_as, W_ah, ba, v, W_a, out):
             if t == 0:
                 nc.scalar.copy(out=m[:, bt, :], in_=z[:])
             else:
-                nc.vector.tensor_tensor(out=m[:, bt, :], in0=z[:], in1=m[:, bt, :], op=ALU.max)
+                for lo in (0, 256):
+                    nc.vector.tensor_tensor(
+                        out=m[:, bt, lo : lo + 256], in0=z[:, lo : lo + 256], in1=m[:, bt, lo : lo + 256],
+                        op=ALU.max,
+                    )
 
         def subtract(bt, t):
             nc.vector.tensor_tensor(
@@ -269,6 +272,11 @@ def tile_haint_attention_kernel(tc, ht, ct, hi, W_as, W_ah, ba, v, W_a, out):
             copy(out=o_sb[:, bt, :], in_=o_ps[:].rearrange("p c h -> p (c h)"))
             nc.sync.dma_start(out=out[P * bt : P * (bt + 1), :], in_=o_sb[:, bt, :])
 
+        idle_bank = psz.tile([P, H], F32, tag="z")
+
+        def warm_up(words):
+            nc.tensor.matmul(out=idle_bank[:, 0:256], lhsT=ident_f[:], rhs=words, start=True, stop=True)
+
         w_regroup(1, V_COLS)
         w_regroup(2, V_COLS)
         w_quantise(1)
@@ -278,8 +286,12 @@ def tile_haint_attention_kernel(tc, ht, ct, hi, W_as, W_ah, ba, v, W_a, out):
         pb = psw.tile([P, P], BF16, tag="w")
         nc.tensor.transpose(pb[:], ba16[:], ident_b[:])
         nc.vector.tensor_copy(out=ba_sb[:], in_=pb[:, 0:4])
+        warm_up(was_raw[:].bitcast(F32)[:, 0:256])
+        warm_up(was_raw[:].bitcast(F32)[:, 1024:1280])
+        warm_up(wah_raw[:].bitcast(F32)[:, 0:256])
         q_rows(0)
         hi_rows(0, 0, 2)
+        warm_up(q_grp32[:, 0:256])
         q_quantise(0)
         hi_quantise(0, 0, 2)
         hi_rows(0, 2, 2)
@@ -315,30 +327,17 @@ def tile_haint_attention_kernel(tc, ht, ct, hi, W_as, W_ah, ba, v, W_a, out):
             g_quantise(1, t0, count)
             if 2 * u + 1 < T:
                 subtract(0, 2 * u + 1)
-        stage2(1, 0)
-        stage2(1, 1)
-        exponent(0, 0)
-        product(0, 0)
-        exponent(0, 1)
-        product(0, 1)
+        for t in range(T):
+            stage2(1, t)
+
         open_sum(0, 0)
-        add_to_sum(0, 0, 0)
-        stage2(1, 2)
-        exponent(0, 2)
-        product(0, 2)
-        add_to_sum(0, 0, 1)
-        stage2(1, 3)
-        exponent(0, 3)
-        product(0, 3)
-        add_to_sum(0, 0, 2)
-        add_to_sum(0, 0, 3)
-        stage2(1, 4)
-        exponent(0, 4)
-        product(0, 4)
-        add_to_sum(0, 0, 4)
+        for t in range(T):
+            exponent(0, t)
+            product(0, t)
+            add_to_sum(0, 0, t)
         square_sum(0)
         open_sum(0, 1)
-        for t in range(3):
+        for t in range(T):
             add_to_sum(0, 1, t)
 
         for t in range(T):
@@ -346,31 +345,15 @@ def tile_haint_attention_kernel(tc, ht, ct, hi, W_as, W_ah, ba, v, W_a, out):
         open_sum(1, 0)
         for t in range(T):
             exponent(1, t)
-            if t in MUL_ON_G[1]:
-                product(1, t)
             add_to_sum(1, 0, t)
-            if 1 <= t <= 2:
-                add_to_sum(0, 1, t + 2)
+        open_sum(1, 1)
+        for t in range(T):
+            product(1, t)
+            add_to_sum(1, 1, t)
         one_over(0)
         square_sum(1)
         one_over(1)
-
-        def add(dst, a, b):
-            nc.vector.tensor_tensor(out=dst, in0=a, in1=b, op=ALU.add)
-
-        product(1, 2)
-        product(1, 3)
-        add(part[:, 0, :], w[:, T + 2, :], w[:, T + 3, :])
-        product(1, 4)
-        add(part[:, 0, :], part[:, 0, :], w[:, T + 4, :])
-        add(part[:, 1, :], w[:, T, :], w[:, T + 1, :])
         normalise(0)
-        add(part[:, 0, :], part[:, 0, :], part[:, 1, :])
         store(0)
-        r_ps = psz.tile([P, 4, P], F32, tag="z")
-        for c in range(4):
-            nc.tensor.transpose(r_ps[:, c, :], r[:, 1, P * c : P * (c + 1)], ident_f[:])
-        nc.vector.tensor_tensor(
-            out=o_sb[:, 1, :], in0=r_ps[:].rearrange("p c h -> p (c h)"), in1=part[:, 0, :], op=ALU.mult
-        )
-        nc.sync.dma_start(out=out[P : 2 * P, :], in_=o_sb[:, 1, :])
+        normalise(1)
+        store(1)

@@ -96,6 +96,16 @@ def tile_haint_attention_kernel(tc, ht, ct, hi, W_as, W_ah, ba, v, W_a, out):
                         in_=src[:, :, lo:hi_c].rearrange("p t (c i) -> p c t i", i=4),
                     )
 
+        def wa_regroup():
+            src = raws[3].rearrange("p (t u q i e) -> p u e q t i", t=4, u=2, i=4, e=2)
+            for u in range(2):
+                for ee in range(2):
+                    lo = 2048 * 3 + 512 * (2 * u + ee)
+                    nc.vector.tensor_copy(
+                        out=w_grp[:, lo : lo + 512].rearrange("p (q i t) -> p q t i", i=4, t=4),
+                        in_=src[:, u, ee, :, :, :],
+                    )
+
         def w_quantise(i):
             quantise(
                 w_codes[:, 512 * i : 512 * (i + 1)],
@@ -202,14 +212,17 @@ def tile_haint_attention_kernel(tc, ht, ct, hi, W_as, W_ah, ba, v, W_a, out):
         w = keep.tile([P, NBT * T, H], F32)
         s2 = keep.tile([P, NBT, H], F32)
         r = keep.tile([P, NBT, H], F32)
-        oT = keep.tile([P, NBT, 4, P], F32)
         o_sb = keep.tile([P, NBT, H], F32)
         zs = {}
         sums = {}
 
         def stage2(bt, t):
             z = psz.tile([P, H], F32, tag="z")
-            mx(z[:], g_codes, g_scales, P * (T * bt + t), w_codes, w_scales, 1536, 512, True, True)
+            for j in range(4):
+                mx(
+                    z[:, P * j : P * (j + 1)], w_codes, w_scales, 1536 + P * j,
+                    g_codes, g_scales, P * (T * bt + t), P, True, True,
+                )
             zs[(bt, t)] = z
             if t == 0:
                 nc.scalar.copy(out=m[:, bt, :], in_=z[:])
@@ -232,7 +245,9 @@ def tile_haint_attention_kernel(tc, ht, ct, hi, W_as, W_ah, ba, v, W_a, out):
             k = T * bt + t
             eng = nc.gpsimd if t in MUL_ON_G[bt] else nc.vector
             eng.tensor_tensor(
-                out=w[:, k, :], in0=e[:, k, :], in1=hi_sb[:, H * k : H * (k + 1)], op=ALU.mult
+                out=w[:, k, :].rearrange("p (j b) -> p j b", j=4),
+                in0=e[:, k, :].rearrange("p (j b) -> p j b", j=4),
+                in1=hi_grp[:, H * k : H * (k + 1)].rearrange("p (b j) -> p j b", j=4), op=ALU.mult,
             )
 
         def open_sum(bt, what):
@@ -249,9 +264,13 @@ def tile_haint_attention_kernel(tc, ht, ct, hi, W_as, W_ah, ba, v, W_a, out):
                     start=(t == 0 and c == 0), stop=(t == T - 1 and c == 3),
                 )
 
+        def natural(ap):
+            return ap.rearrange("p (u e) q -> p u q e", u=2)
+
         def square_sum(bt):
             nc.scalar.activation(
-                out=s2[:, bt, :], in_=sums[(bt, 0)][:].rearrange("p c b -> p (c b)"), func=AF.Square
+                out=s2[:, bt, :].rearrange("p (u q e) -> p u q e", u=2, e=2),
+                in_=natural(sums[(bt, 0)][:]), func=AF.Square,
             )
 
         def one_over(bt):
@@ -259,17 +278,12 @@ def tile_haint_attention_kernel(tc, ht, ct, hi, W_as, W_ah, ba, v, W_a, out):
 
         def normalise(bt):
             nc.vector.tensor_tensor(
-                out=oT[:, bt, :, :].rearrange("p c b -> p (c b)"),
-                in0=sums[(bt, 1)][:].rearrange("p c b -> p (c b)"), in1=r[:, bt, :], op=ALU.mult,
+                out=o_sb[:, bt, :].rearrange("p (u q e) -> p u q e", u=2, e=2),
+                in0=natural(sums[(bt, 1)][:]),
+                in1=r[:, bt, :].rearrange("p (u q e) -> p u q e", u=2, e=2), op=ALU.mult,
             )
 
         def store(bt):
-            pool, tag = ((psw, "w"), (psz, "z"))[bt]
-            o_ps = pool.tile([P, 4, P], F32, tag=tag)
-            for c in range(4):
-                nc.tensor.transpose(o_ps[:, c, :], oT[:, bt, c, :], ident_f[:])
-            copy = (nc.scalar.copy, nc.vector.tensor_copy)[bt]
-            copy(out=o_sb[:, bt, :], in_=o_ps[:].rearrange("p c h -> p (c h)"))
             nc.sync.dma_start(out=out[P * bt : P * (bt + 1), :], in_=o_sb[:, bt, :])
 
         idle_bank = psz.tile([P, H], F32, tag="z")
@@ -296,7 +310,7 @@ def tile_haint_attention_kernel(tc, ht, ct, hi, W_as, W_ah, ba, v, W_a, out):
         hi_quantise(0, 0, 2)
         hi_rows(0, 2, 2)
         hi_rows(0, 4, 1)
-        w_regroup(3, 512)
+        wa_regroup()
         hi_quantise(0, 2, 2)
         w_quantise(3)
         hi_quantise(0, 4, 1)

@@ -21,8 +21,8 @@ A = 512
 
 PIN = True
 V_COLS = 352
-MUL_ON_G = ((0, 1, 2, 3, 4), ())
-UNITS = ((0, 2), (2, 2), (4, 1))
+MUL_ON_G = ((0, 1, 2, 3, 4), (0, 2))
+WARM = 2
 
 
 def tile_haint_attention_kernel(tc, ht, ct, hi, W_as, W_ah, ba, v, W_a, out):
@@ -31,7 +31,8 @@ def tile_haint_attention_kernel(tc, ht, ct, hi, W_as, W_ah, ba, v, W_a, out):
         if PIN:
             ctx.enter_context(tc.manual_schedule())
         keep = ctx.enter_context(tc.tile_pool(name="keep", bufs=1))
-        psw = ctx.enter_context(tc.psum_pool(name="psw", bufs=3))
+        psa = ctx.enter_context(tc.psum_pool(name="psa", bufs=2))
+        psw = ctx.enter_context(tc.psum_pool(name="psw", bufs=1))
         psz = ctx.enter_context(tc.psum_pool(name="psz", bufs=5))
 
         ident_f = keep.tile([P, P], F32)
@@ -66,9 +67,9 @@ def tile_haint_attention_kernel(tc, ht, ct, hi, W_as, W_ah, ba, v, W_a, out):
         nc.scalar.dma_start(out=ba16[0:4, :], in_=ba.rearrange("o (j p) -> (o j) p", p=P))
         load_k_pairs(was_raw[:, 0 : 4 * A], W_as[0:512, :])
         load_k_pairs(was_raw[:, 4 * A : 8 * A], W_as[512:1024, :])
-        load_k_pairs(wah_raw[:], W_ah)
         load_q(0)
         load_hi(0, 0, 2)
+        load_k_pairs(wah_raw[:], W_ah)
         load_hi(0, 2, 5)
         nc.sync.dma_start(
             out=wa_raw[:].rearrange("p (t n) -> p t n", t=4),
@@ -124,8 +125,8 @@ def tile_haint_attention_kernel(tc, ht, ct, hi, W_as, W_ah, ba, v, W_a, out):
         q_grp32 = q_grp[:].bitcast(F32)
         hi_grp32 = hi_grp[:].bitcast(F32)
 
-        def transpose_words(src32, dst32, first, count):
-            xt = psw.tile([P, 4, P], F32, tag="w")
+        def transpose_words(pool, tag, src32, dst32, first, count):
+            xt = pool.tile([P, 4, P], F32, tag=tag)
             for i in range(2 * count):
                 nc.tensor.transpose(
                     xt[:, i, :], src32[:, 256 * first + P * i : 256 * first + P * (i + 1)], ident_f[:]
@@ -137,8 +138,8 @@ def tile_haint_attention_kernel(tc, ht, ct, hi, W_as, W_ah, ba, v, W_a, out):
                 in_=xt[:, 0 : 2 * count, :].rearrange("p (g u) b -> p g b u", u=2),
             )
 
-        def q_rows(bt):
-            transpose_words(q32, q_grp32, 2 * bt, 2)
+        def q_rows(bt, pool, tag):
+            transpose_words(pool, tag, q32, q_grp32, 2 * bt, 2)
 
         def q_quantise(bt):
             quantise(
@@ -146,8 +147,8 @@ def tile_haint_attention_kernel(tc, ht, ct, hi, W_as, W_ah, ba, v, W_a, out):
                 q_grp[:, 1024 * bt : 1024 * (bt + 1)],
             )
 
-        def hi_rows(bt, t0, count):
-            transpose_words(hi32, hi_grp32, T * bt + t0, count)
+        def hi_rows(bt, t0, count, pool, tag):
+            transpose_words(pool, tag, hi32, hi_grp32, T * bt + t0, count)
 
         def hi_quantise(bt, t0, count):
             c0 = P * (T * bt + t0)
@@ -178,19 +179,21 @@ def tile_haint_attention_kernel(tc, ht, ct, hi, W_as, W_ah, ba, v, W_a, out):
             mx(o, w_codes, w_scales, 512 + P * j, q_codes, q_scales, P * (2 * bt), P, False, False)
             mx(o, w_codes, w_scales, 1024 + P * j, q_codes, q_scales, P * (2 * bt + 1), P, False, True)
 
-        def stage1(bt, t0, count):
-            c0 = P * (T * bt + t0)
-            j_per_bank = 4 // count
-            for j0 in range(0, 4, j_per_bank):
-                acc = psw.tile([P, j_per_bank, count * P], F32, tag="w")
-                for jj in range(j_per_bank):
-                    for tt in range(count):
-                        stage1_group(acc[:, jj, P * tt : P * (tt + 1)], bt, j0 + jj, t0 + tt)
-                for jj in range(j_per_bank):
-                    nc.scalar.activation(
-                        out=gt[:, j0 + jj, c0 : c0 + P * count], in_=acc[:, jj, :],
-                        func=AF.Tanh, bias=ba_sb[:, j0 + jj : j0 + jj + 1], scale=1.0,
-                    )
+        accs = {}
+
+        def stage1(bt, t):
+            acc = psa.tile([P, 4, P], F32, tag="a")
+            for j in range(4):
+                stage1_group(acc[:, j, :], bt, j, t)
+            accs[(bt, t)] = acc
+
+        def tanh(bt, t):
+            c0 = P * (T * bt + t)
+            for j in range(4):
+                nc.scalar.activation(
+                    out=gt[:, j, c0 : c0 + P], in_=accs[(bt, t)][:, j, :],
+                    func=AF.Tanh, bias=ba_sb[:, j : j + 1], scale=1.0,
+                )
 
         def g_regroup(bt, t0, count):
             c0 = P * (T * bt + t0)
@@ -224,14 +227,13 @@ def tile_haint_attention_kernel(tc, ht, ct, hi, W_as, W_ah, ba, v, W_a, out):
                     g_codes, g_scales, P * (T * bt + t), P, True, True,
                 )
             zs[(bt, t)] = z
+
+        def maximum(bt, t):
+            z = zs[(bt, t)]
             if t == 0:
                 nc.scalar.copy(out=m[:, bt, :], in_=z[:])
             else:
-                for lo in (0, 256):
-                    nc.vector.tensor_tensor(
-                        out=m[:, bt, lo : lo + 256], in0=z[:, lo : lo + 256], in1=m[:, bt, lo : lo + 256],
-                        op=ALU.max,
-                    )
+                nc.vector.tensor_tensor(out=m[:, bt, :], in0=z[:], in1=m[:, bt, :], op=ALU.max)
 
         def subtract(bt, t):
             nc.vector.tensor_tensor(
@@ -292,82 +294,99 @@ def tile_haint_attention_kernel(tc, ht, ct, hi, W_as, W_ah, ba, v, W_a, out):
             nc.tensor.matmul(out=idle_bank[:, 0:256], lhsT=ident_f[:], rhs=words, start=True, stop=True)
 
         w_regroup(1, V_COLS)
-        w_regroup(2, V_COLS)
         w_quantise(1)
-        w_regroup(0, V_COLS)
-        w_quantise(2)
-        w_quantise(0)
+        w_regroup(2, V_COLS)
         pb = psw.tile([P, P], BF16, tag="w")
         nc.tensor.transpose(pb[:], ba16[:], ident_b[:])
+        q_rows(0, psa, "a")
+        hi_rows(0, 0, 2, psa, "a")
+        w_quantise(2)
         nc.vector.tensor_copy(out=ba_sb[:], in_=pb[:, 0:4])
-        warm_up(was_raw[:].bitcast(F32)[:, 0:256])
-        warm_up(was_raw[:].bitcast(F32)[:, 1024:1280])
-        warm_up(wah_raw[:].bitcast(F32)[:, 0:256])
-        q_rows(0)
-        hi_rows(0, 0, 2)
-        warm_up(q_grp32[:, 0:256])
         q_quantise(0)
+        w_regroup(0, V_COLS)
         hi_quantise(0, 0, 2)
-        hi_rows(0, 2, 2)
-        hi_rows(0, 4, 1)
-        wa_regroup()
+        w_quantise(0)
+        for k in range(WARM):
+            warm_up(was_raw[:].bitcast(F32)[:, 256 * k : 256 * (k + 1)])
+        hi_rows(0, 2, 2, psa, "a")
         hi_quantise(0, 2, 2)
-        w_quantise(3)
-        hi_quantise(0, 4, 1)
 
-        for t0, count in UNITS:
-            stage1(0, t0, count)
-            g_regroup(0, t0, count)
-            g_quantise(0, t0, count)
+        rows1 = {1: lambda: q_rows(1, psw, "w"), 2: lambda: hi_rows(1, 0, 2, psw, "w"), 3: lambda: hi_rows(1, 2, 2, psw, "w"), 4: lambda: hi_rows(1, 4, 1, psw, "w")}
+        quants1 = {2: lambda: q_quantise(1), 3: lambda: hi_quantise(1, 0, 2), 4: lambda: hi_quantise(1, 2, 2), 5: lambda: hi_quantise(1, 4, 1)}
 
-        q_rows(1)
-        hi_rows(1, 0, 2)
-        q_quantise(1)
-        hi_quantise(1, 0, 2)
-        for t in range(3):
-            stage2(0, t)
-        hi_rows(1, 2, 2)
-        hi_rows(1, 4, 1)
-        hi_quantise(1, 2, 2)
-        hi_quantise(1, 4, 1)
-        for t in range(3, T):
-            stage2(0, t)
+        def zmat(i):
+            stage2(i // T, i % T)
 
-        for u in range(3):
-            t0, count = UNITS[u]
-            stage1(1, t0, count)
-            g_regroup(1, t0, count)
-            subtract(0, 2 * u)
-            g_quantise(1, t0, count)
-            if 2 * u + 1 < T:
-                subtract(0, 2 * u + 1)
-        for t in range(T):
-            stage2(1, t)
+        def vmax(i):
+            maximum(i // T, i % T)
 
+        for s in range(10):
+            if 3 <= s < 8:
+                vmax(s - 3)
+            if s == 7:
+                subtract(0, 0)
+            stage1(s // T, s % T)
+            tanh(s // T, s % T)
+            if s == 0:
+                hi_rows(0, 4, 1, psw, "w")
+                wa_regroup()
+                w_quantise(3)
+            if s in rows1:
+                rows1[s]()
+            if s >= 1:
+                g_regroup((s - 1) // T, (s - 1) % T, 1)
+            if s == 1:
+                hi_quantise(0, 4, 1)
+            if s in quants1:
+                quants1[s]()
+            if s >= 7:
+                subtract(0, s - 6)
+            if s >= 1:
+                g_quantise((s - 1) // T, (s - 1) % T, 1)
+            if 2 <= s < 7:
+                zmat(s - 2)
+            if s >= 7:
+                exponent(0, s - 7)
+                product(0, s - 7)
+            if s >= 8:
+                zmat(s - 3)
+                vmax(s - 3)
         open_sum(0, 0)
-        for t in range(T):
-            exponent(0, t)
-            product(0, t)
-            add_to_sum(0, 0, t)
+        add_to_sum(0, 0, 0)
+        g_regroup(1, 4, 1)
+        subtract(0, 4)
+        g_quantise(1, 4, 1)
+        zmat(7)
+        add_to_sum(0, 0, 1)
+        vmax(7)
+        exponent(0, 3)
+        product(0, 3)
+        zmat(8)
+        add_to_sum(0, 0, 2)
+        vmax(8)
+        exponent(0, 4)
+        product(0, 4)
+        zmat(9)
+        add_to_sum(0, 0, 3)
+        vmax(9)
+        add_to_sum(0, 0, 4)
         square_sum(0)
+        one_over(0)
         open_sum(0, 1)
         for t in range(T):
-            add_to_sum(0, 1, t)
-
-        for t in range(T):
             subtract(1, t)
+            exponent(1, t)
+            add_to_sum(0, 1, t)
         open_sum(1, 0)
         for t in range(T):
-            exponent(1, t)
             add_to_sum(1, 0, t)
-        open_sum(1, 1)
-        for t in range(T):
             product(1, t)
-            add_to_sum(1, 1, t)
-        one_over(0)
         square_sum(1)
         one_over(1)
         normalise(0)
         store(0)
+        open_sum(1, 1)
+        for t in range(T):
+            add_to_sum(1, 1, t)
         normalise(1)
         store(1)

@@ -288,9 +288,8 @@ def tile_haint_attention_kernel(tc, ht, ct, hi, W_as, W_ah, ba, v, W_a, out):
         def store(bt):
             nc.sync.dma_start(out=out[P * bt : P * (bt + 1), :], in_=o_sb[:, bt, :])
 
-        idle_bank = psz.tile([P, H], F32, tag="z")
-
         def warm_up(words):
+            idle_bank = psa.tile([P, H], F32, tag="a")
             nc.tensor.matmul(out=idle_bank[:, 0:256], lhsT=ident_f[:], rhs=words, start=True, stop=True)
 
         w_regroup(1, V_COLS)
@@ -371,16 +370,19 @@ def tile_haint_attention_kernel(tc, ht, ct, hi, W_as, W_ah, ba, v, W_a, out):
         vmax(9)
         add_to_sum(0, 0, 4)
         square_sum(0)
-        one_over(0)
         open_sum(0, 1)
+        warm_up(was_raw[:].bitcast(F32)[:, 0:256])
         for t in range(T):
             subtract(1, t)
             exponent(1, t)
             add_to_sum(0, 1, t)
         open_sum(1, 0)
+        warm_up(was_raw[:].bitcast(F32)[:, 0:256])
         for t in range(T):
             add_to_sum(1, 0, t)
             product(1, t)
+        warm_up(was_raw[:].bitcast(F32)[:, 0:256])
+        one_over(0)
         square_sum(1)
         one_over(1)
         normalise(0)

@@ -21,7 +21,7 @@ A = 512
 
 PIN = True
 V_COLS = 352
-MUL_ON_G = ((0, 1, 2, 3, 4), (0, 2))
+MUL_ON_G = ((), ())
 WARM = 2
 
 

@@ -21,8 +21,7 @@ A = 512
 
 PIN = True
 V_COLS = 352
-MUL_ON_G = ((), ())
-WARM = 2
+MUL_ON_G = ((0, 1, 2, 3), ())
 
 
 def tile_haint_attention_kernel(tc, ht, ct, hi, W_as, W_ah, ba, v, W_a, out):
@@ -67,10 +66,10 @@ def tile_haint_attention_kernel(tc, ht, ct, hi, W_as, W_ah, ba, v, W_a, out):
         nc.scalar.dma_start(out=ba16[0:4, :], in_=ba.rearrange("o (j p) -> (o j) p", p=P))
         load_k_pairs(was_raw[:, 0 : 4 * A], W_as[0:512, :])
         load_k_pairs(was_raw[:, 4 * A : 8 * A], W_as[512:1024, :])
-        load_q(0)
-        load_hi(0, 0, 2)
         load_k_pairs(wah_raw[:], W_ah)
-        load_hi(0, 2, 5)
+        load_q(0)
+        load_hi(0, 0, 1)
+        load_hi(0, 1, 5)
         nc.sync.dma_start(
             out=wa_raw[:].rearrange("p (t n) -> p t n", t=4),
             in_=W_a.rearrange("(t p) n -> p t n", p=P),
@@ -86,9 +85,9 @@ def tile_haint_attention_kernel(tc, ht, ct, hi, W_as, W_ah, ba, v, W_a, out):
         def quantise(codes, scales, src):
             nc.vector.quantize_mx(out=codes.bitcast(FP8X4), scales=scales, in_=src)
 
-        def w_regroup(i, v_cols):
+        def w_regroup(i, v_cols, s_end=512):
             src = raws[i].rearrange("p (t c) -> p t c", t=4)
-            for copy, lo, hi_c in ((nc.vector.tensor_copy, 0, v_cols), (nc.scalar.copy, v_cols, 512)):
+            for copy, lo, hi_c in ((nc.vector.tensor_copy, 0, v_cols), (nc.scalar.copy, v_cols, s_end)):
                 if hi_c > lo:
                     copy(
                         out=w_grp[:, 2048 * i + 4 * lo : 2048 * i + 4 * hi_c].rearrange(
@@ -96,6 +95,18 @@ def tile_haint_attention_kernel(tc, ht, ct, hi, W_as, W_ah, ba, v, W_a, out):
                         ),
                         in_=src[:, :, lo:hi_c].rearrange("p t (c i) -> p c t i", i=4),
                     )
+
+        def w_identity(i, lo, cols):
+            ps = psa.tile([P, 4, cols], BF16, tag="a")
+            for t in range(4):
+                nc.tensor.matmul(
+                    out=ps[:, t, :], lhsT=ident_b[:], rhs=raws[i][:, 512 * t + lo : 512 * t + lo + cols],
+                    start=True, stop=True,
+                )
+            nc.scalar.copy(
+                out=w_grp[:, 2048 * i + 4 * lo : 2048 * i + 4 * (lo + cols)].rearrange("p (c t) -> p c t", t=4),
+                in_=ps[:].rearrange("p t c -> p c t"),
+            )
 
         def wa_regroup():
             src = raws[3].rearrange("p (t u q i e) -> p u e q t i", t=4, u=2, i=4, e=2)
@@ -233,7 +244,12 @@ def tile_haint_attention_kernel(tc, ht, ct, hi, W_as, W_ah, ba, v, W_a, out):
             if t == 0:
                 nc.scalar.copy(out=m[:, bt, :], in_=z[:])
             else:
-                nc.vector.tensor_tensor(out=m[:, bt, :], in0=z[:], in1=m[:, bt, :], op=ALU.max)
+                step = 256 if bt else 512
+                for lo in range(0, 512, step):
+                    nc.vector.tensor_tensor(
+                        out=m[:, bt, lo : lo + step], in0=z[:, lo : lo + step], in1=m[:, bt, lo : lo + step],
+                        op=ALU.max,
+                    )
 
         def subtract(bt, t):
             nc.vector.tensor_tensor(
@@ -253,17 +269,18 @@ def tile_haint_attention_kernel(tc, ht, ct, hi, W_as, W_ah, ba, v, W_a, out):
             )
 
         def open_sum(bt, what):
-            pool, tag = ((psw, "w"), (psz, "z"))[bt]
+            pool, tag = ((psw, "w") if what == 0 else (psa, "a"), (psz, "z"))[bt]
             acc_t = pool.tile([P, 4, P], F32, tag=tag)
             sums[(bt, what)] = acc_t
 
-        def add_to_sum(bt, what, t):
+        def add_to_sum(bt, what, t, place=None):
+            place = t if place is None else place
             src = (e, w)[what]
             for c in range(4):
                 nc.tensor.matmul(
                     out=sums[(bt, what)][:, c, :], lhsT=src[:, T * bt + t, P * c : P * (c + 1)],
                     rhs=ident_f[:], is_transpose=True,
-                    start=(t == 0 and c == 0), stop=(t == T - 1 and c == 3),
+                    start=(place == 0 and c == 0), stop=(place == T - 1 and c == 3),
                 )
 
         def natural(ap):
@@ -288,30 +305,27 @@ def tile_haint_attention_kernel(tc, ht, ct, hi, W_as, W_ah, ba, v, W_a, out):
         def store(bt):
             nc.sync.dma_start(out=out[P * bt : P * (bt + 1), :], in_=o_sb[:, bt, :])
 
-        def warm_up(words):
-            idle_bank = psa.tile([P, H], F32, tag="a")
-            nc.tensor.matmul(out=idle_bank[:, 0:256], lhsT=ident_f[:], rhs=words, start=True, stop=True)
+        def warm_up(idle_bank, n):
+            nc.tensor.matmul(out=idle_bank[:, 0:n], lhsT=ident_f[:], rhs=hi32[:, 0:n], start=True, stop=True)
 
-        w_regroup(1, V_COLS)
+        w_identity(1, 256, 256)
+        w_regroup(1, 256, 256)
+        w_identity(2, 256, 256)
+        w_regroup(2, 256, 256)
         w_quantise(1)
-        w_regroup(2, V_COLS)
         pb = psw.tile([P, P], BF16, tag="w")
         nc.tensor.transpose(pb[:], ba16[:], ident_b[:])
-        q_rows(0, psa, "a")
-        hi_rows(0, 0, 2, psa, "a")
+        w_identity(0, 256, 256)
+        w_regroup(0, 256, 256)
         w_quantise(2)
         nc.vector.tensor_copy(out=ba_sb[:], in_=pb[:, 0:4])
-        q_quantise(0)
-        w_regroup(0, V_COLS)
-        hi_quantise(0, 0, 2)
+        q_rows(0, psz, "z")
+        hi_rows(0, 0, 1, psz, "z")
         w_quantise(0)
-        for k in range(WARM):
-            warm_up(was_raw[:].bitcast(F32)[:, 256 * k : 256 * (k + 1)])
-        hi_rows(0, 2, 2, psa, "a")
-        hi_quantise(0, 2, 2)
-
-        rows1 = {1: lambda: q_rows(1, psw, "w"), 2: lambda: hi_rows(1, 0, 2, psw, "w"), 3: lambda: hi_rows(1, 2, 2, psw, "w"), 4: lambda: hi_rows(1, 4, 1, psw, "w")}
-        quants1 = {2: lambda: q_quantise(1), 3: lambda: hi_quantise(1, 0, 2), 4: lambda: hi_quantise(1, 2, 2), 5: lambda: hi_quantise(1, 4, 1)}
+        q_quantise(0)
+        hi_quantise(0, 0, 1)
+        hi_rows(0, 1, 2, psz, "z")
+        hi_quantise(0, 1, 2)
 
         def zmat(i):
             stage2(i // T, i % T)
@@ -319,69 +333,114 @@ def tile_haint_attention_kernel(tc, ht, ct, hi, W_as, W_ah, ba, v, W_a, out):
         def vmax(i):
             maximum(i // T, i % T)
 
-        for s in range(10):
-            if 3 <= s < 8:
-                vmax(s - 3)
-            if s == 7:
-                subtract(0, 0)
-            stage1(s // T, s % T)
-            tanh(s // T, s % T)
-            if s == 0:
-                hi_rows(0, 4, 1, psw, "w")
-                wa_regroup()
-                w_quantise(3)
-            if s in rows1:
-                rows1[s]()
-            if s >= 1:
-                g_regroup((s - 1) // T, (s - 1) % T, 1)
-            if s == 1:
-                hi_quantise(0, 4, 1)
-            if s in quants1:
-                quants1[s]()
-            if s >= 7:
-                subtract(0, s - 6)
-            if s >= 1:
-                g_quantise((s - 1) // T, (s - 1) % T, 1)
-            if 2 <= s < 7:
-                zmat(s - 2)
-            if s >= 7:
-                exponent(0, s - 7)
-                product(0, s - 7)
-            if s >= 8:
-                zmat(s - 3)
-                vmax(s - 3)
+        def s1(i):
+            stage1(i // T, i % T)
+            tanh(i // T, i % T)
+
+        def rg(i):
+            g_regroup(i // T, i % T, 1)
+
+        def gq(i):
+            g_quantise(i // T, i % T, 1)
+
+        s1(0)
+        hi_rows(0, 3, 2, psz, "z")
+        wa_regroup()
+        w_quantise(3)
+        s1(1)
+        q_rows(1, psz, "z")
+        rg(0)
+        hi_quantise(0, 3, 2)
+        gq(0)
+        s1(2)
+        hi_rows(1, 0, 2, psz, "z")
+        rg(1)
+        q_quantise(1)
+        gq(1)
+        zmat(0)
+        vmax(0)
+        s1(3)
+        hi_rows(1, 2, 2, psz, "z")
+        rg(2)
+        hi_quantise(1, 0, 2)
+        gq(2)
+        zmat(1)
+        s1(4)
+        vmax(1)
+        hi_rows(1, 4, 1, psw, "w")
+        rg(3)
+        hi_quantise(1, 2, 2)
+        gq(3)
+        zmat(2)
+        s1(5)
+        vmax(2)
+        zmat(3)
+        rg(4)
+        hi_quantise(1, 4, 1)
+        gq(4)
+        vmax(3)
+        s1(6)
+        zmat(4)
+        rg(5)
+        vmax(4)
+        gq(5)
+        subtract(0, 0)
+        s1(7)
+        rg(6)
+        subtract(0, 1)
+        gq(6)
+        zmat(5)
+        s1(8)
+        vmax(5)
+        rg(7)
+        subtract(0, 2)
+        gq(7)
+        zmat(6)
+        s1(9)
+        rg(8)
+        vmax(6)
+        gq(8)
+        subtract(0, 3)
+        zmat(7)
+
+        rg(9)
+        exponent(0, 0)
+        exponent(0, 1)
+        exponent(0, 2)
+        exponent(0, 3)
+        vmax(7)
+        gq(9)
+        subtract(0, 4)
+        product(0, 3)
+        product(0, 0)
+        product(0, 1)
+        product(0, 2)
+        exponent(0, 4)
         open_sum(0, 0)
         add_to_sum(0, 0, 0)
-        g_regroup(1, 4, 1)
-        subtract(0, 4)
-        g_quantise(1, 4, 1)
-        zmat(7)
         add_to_sum(0, 0, 1)
-        vmax(7)
-        exponent(0, 3)
-        product(0, 3)
         zmat(8)
-        add_to_sum(0, 0, 2)
         vmax(8)
-        exponent(0, 4)
-        product(0, 4)
         zmat(9)
-        add_to_sum(0, 0, 3)
         vmax(9)
+        add_to_sum(0, 0, 2)
+        add_to_sum(0, 0, 3)
         add_to_sum(0, 0, 4)
         square_sum(0)
-        open_sum(0, 1)
-        warm_up(was_raw[:].bitcast(F32)[:, 0:256])
+        idle = psa.tile([P, H], F32, tag="a", name="idle_tail")
+        warm_up(idle, 256)
         for t in range(T):
             subtract(1, t)
             exponent(1, t)
-            add_to_sum(0, 1, t)
+        product(0, 4)
+        open_sum(0, 1)
         open_sum(1, 0)
-        warm_up(was_raw[:].bitcast(F32)[:, 0:256])
+        for n, t in enumerate((3, 0, 1, 2, 4)):
+            add_to_sum(0, 1, t, n)
+            add_to_sum(1, 0, n)
+            warm_up(idle, 128)
         for t in range(T):
-            add_to_sum(1, 0, t)
             product(1, t)
-        warm_up(was_raw[:].bitcast(F32)[:, 0:256])
         one_over(0)
         square_sum(1)
         one_over(1)
@@ -390,5 +449,7 @@ def tile_haint_attention_kernel(tc, ht, ct, hi, W_as, W_ah, ba, v, W_a, out):
         open_sum(1, 1)
         for t in range(T):
             add_to_sum(1, 1, t)
+            if t in (1, 3):
+                warm_up(idle, 128)
         normalise(1)
         store(1)

@@ -308,15 +308,12 @@ def tile_haint_attention_kernel(tc, ht, ct, hi, W_as, W_ah, ba, v, W_a, out):
         def warm_up(idle_bank, n):
             nc.tensor.matmul(out=idle_bank[:, 0:n], lhsT=ident_f[:], rhs=hi32[:, 0:n], start=True, stop=True)
 
-        w_identity(1, 256, 256)
-        w_regroup(1, 256, 256)
-        w_identity(2, 256, 256)
-        w_regroup(2, 256, 256)
+        w_regroup(1, 320)
+        w_regroup(2, 320)
         w_quantise(1)
         pb = psw.tile([P, P], BF16, tag="w")
         nc.tensor.transpose(pb[:], ba16[:], ident_b[:])
-        w_identity(0, 256, 256)
-        w_regroup(0, 256, 256)
+        w_regroup(0, 320)
         w_quantise(2)
         nc.vector.tensor_copy(out=ba_sb[:], in_=pb[:, 0:4])
         q_rows(0, psz, "z")
@@ -438,7 +435,8 @@ def tile_haint_attention_kernel(tc, ht, ct, hi, W_as, W_ah, ba, v, W_a, out):
         for n, t in enumerate((3, 0, 1, 2, 4)):
             add_to_sum(0, 1, t, n)
             add_to_sum(1, 0, n)
-            warm_up(idle, 128)
+            if n in (1, 4):
+                warm_up(idle, 256)
         for t in range(T):
             product(1, t)
         one_over(0)
@@ -449,7 +447,7 @@ def tile_haint_attention_kernel(tc, ht, ct, hi, W_as, W_ah, ba, v, W_a, out):
         open_sum(1, 1)
         for t in range(T):
             add_to_sum(1, 1, t)
-            if t in (1, 3):
-                warm_up(idle, 128)
+            if t in ():
+                warm_up(idle, 256)
         normalise(1)
         store(1)

@@ -22,6 +22,7 @@ A = 512
 PIN = True
 V_COLS = 352
 MUL_ON_G = ((0, 1, 2, 3), ())
+HALVED = ((1, 3), (1, 4))
 
 
 def tile_haint_attention_kernel(tc, ht, ct, hi, W_as, W_ah, ba, v, W_a, out):
@@ -111,9 +112,10 @@ def tile_haint_attention_kernel(tc, ht, ct, hi, W_as, W_ah, ba, v, W_a, out):
         def wa_regroup():
             src = raws[3].rearrange("p (t u q i e) -> p u e q t i", t=4, u=2, i=4, e=2)
             for u in range(2):
+                copy = nc.vector.tensor_copy
                 for ee in range(2):
                     lo = 2048 * 3 + 512 * (2 * u + ee)
-                    nc.vector.tensor_copy(
+                    copy(
                         out=w_grp[:, lo : lo + 512].rearrange("p (q i t) -> p q t i", i=4, t=4),
                         in_=src[:, u, ee, :, :, :],
                     )
@@ -190,21 +192,19 @@ def tile_haint_attention_kernel(tc, ht, ct, hi, W_as, W_ah, ba, v, W_a, out):
             mx(o, w_codes, w_scales, 512 + P * j, q_codes, q_scales, P * (2 * bt), P, False, False)
             mx(o, w_codes, w_scales, 1024 + P * j, q_codes, q_scales, P * (2 * bt + 1), P, False, True)
 
-        accs = {}
-
-        def stage1(bt, t):
-            acc = psa.tile([P, 4, P], F32, tag="a")
-            for j in range(4):
-                stage1_group(acc[:, j, :], bt, j, t)
-            accs[(bt, t)] = acc
-
-        def tanh(bt, t):
-            c0 = P * (T * bt + t)
-            for j in range(4):
-                nc.scalar.activation(
-                    out=gt[:, j, c0 : c0 + P], in_=accs[(bt, t)][:, j, :],
-                    func=AF.Tanh, bias=ba_sb[:, j : j + 1], scale=1.0,
-                )
+        def stage1(bt, t0, count):
+            c0 = P * (T * bt + t0)
+            j_per_bank = 4 // count
+            for j0 in range(0, 4, j_per_bank):
+                acc = psa.tile([P, j_per_bank, count * P], F32, tag="a")
+                for jj in range(j_per_bank):
+                    for tt in range(count):
+                        stage1_group(acc[:, jj, P * tt : P * (tt + 1)], bt, j0 + jj, t0 + tt)
+                for jj in range(j_per_bank):
+                    nc.scalar.activation(
+                        out=gt[:, j0 + jj, c0 : c0 + P * count], in_=acc[:, jj, :],
+                        func=AF.Tanh, bias=ba_sb[:, j0 + jj : j0 + jj + 1], scale=1.0,
+                    )
 
         def g_regroup(bt, t0, count):
             c0 = P * (T * bt + t0)
@@ -244,7 +244,7 @@ def tile_haint_attention_kernel(tc, ht, ct, hi, W_as, W_ah, ba, v, W_a, out):
             if t == 0:
                 nc.scalar.copy(out=m[:, bt, :], in_=z[:])
             else:
-                step = 256 if bt else 512
+                step = 256 if (bt, t) in HALVED else 512
                 for lo in range(0, 512, step):
                     nc.vector.tensor_tensor(
                         out=m[:, bt, lo : lo + step], in0=z[:, lo : lo + step], in1=m[:, bt, lo : lo + step],
@@ -295,15 +295,19 @@ def tile_haint_attention_kernel(tc, ht, ct, hi, W_as, W_ah, ba, v, W_a, out):
         def one_over(bt):
             nc.scalar.activation(out=r[:, bt, :], in_=s2[:, bt, :], func=AF.Abs_reciprocal_sqrt)
 
-        def normalise(bt):
-            nc.vector.tensor_tensor(
-                out=o_sb[:, bt, :].rearrange("p (u q e) -> p u q e", u=2, e=2),
-                in0=natural(sums[(bt, 1)][:]),
-                in1=r[:, bt, :].rearrange("p (u q e) -> p u q e", u=2, e=2), op=ALU.mult,
-            )
+        def finish(bt, halves):
+            for u0, u1 in halves:
+                cols = slice(256 * u0, 256 * u1)
+                nc.vector.tensor_tensor(
+                    out=o_sb[:, bt, cols].rearrange("p (u q e) -> p u q e", e=2, q=P),
+                    in0=natural(sums[(bt, 1)][:])[:, u0:u1, :, :],
+                    in1=r[:, bt, cols].rearrange("p (u q e) -> p u q e", e=2, q=P), op=ALU.mult,
+                )
+                nc.sync.dma_start(out=out[P * bt : P * (bt + 1), cols], in_=o_sb[:, bt, cols])
 
-        def store(bt):
-            nc.sync.dma_start(out=out[P * bt : P * (bt + 1), :], in_=o_sb[:, bt, :])
+        def spin(idle_bank, count):
+            for k in range(count):
+                nc.tensor.matmul(out=idle_bank[:, 0:P], lhsT=ident_f[:], rhs=ident_f[:], start=True, stop=True)
 
         def warm_up(idle_bank, n):
             nc.tensor.matmul(out=idle_bank[:, 0:n], lhsT=ident_f[:], rhs=hi32[:, 0:n], start=True, stop=True)
@@ -316,12 +320,16 @@ def tile_haint_attention_kernel(tc, ht, ct, hi, W_as, W_ah, ba, v, W_a, out):
         w_regroup(0, 320)
         w_quantise(2)
         nc.vector.tensor_copy(out=ba_sb[:], in_=pb[:, 0:4])
+        idle0 = psa.tile([P, H], F32, tag="a", name="idle_head")
+        spin(idle0, 6)
         q_rows(0, psz, "z")
         hi_rows(0, 0, 1, psz, "z")
+        spin(idle0, 3)
         w_quantise(0)
         q_quantise(0)
         hi_quantise(0, 0, 1)
         hi_rows(0, 1, 2, psz, "z")
+        hi_rows(0, 3, 2, psz, "z")
         hi_quantise(0, 1, 2)
 
         def zmat(i):
@@ -330,84 +338,84 @@ def tile_haint_attention_kernel(tc, ht, ct, hi, W_as, W_ah, ba, v, W_a, out):
         def vmax(i):
             maximum(i // T, i % T)
 
-        def s1(i):
-            stage1(i // T, i % T)
-            tanh(i // T, i % T)
+        def s1(i, n=1):
+            stage1(i // T, i % T, n)
 
-        def rg(i):
-            g_regroup(i // T, i % T, 1)
+        def rg(i, n=1):
+            g_regroup(i // T, i % T, n)
 
-        def gq(i):
-            g_quantise(i // T, i % T, 1)
+        def gq(i, n=1):
+            g_quantise(i // T, i % T, n)
 
         s1(0)
-        hi_rows(0, 3, 2, psz, "z")
         wa_regroup()
         w_quantise(3)
-        s1(1)
-        q_rows(1, psz, "z")
-        rg(0)
         hi_quantise(0, 3, 2)
-        gq(0)
+        rg(0)
+        s1(1)
         s1(2)
-        hi_rows(1, 0, 2, psz, "z")
         rg(1)
-        q_quantise(1)
+        gq(0)
         gq(1)
+        q_rows(1, psz, "z")
+        hi_rows(1, 0, 2, psz, "z")
+        rg(2)
+        s1(3)
         zmat(0)
         vmax(0)
-        s1(3)
-        hi_rows(1, 2, 2, psz, "z")
-        rg(2)
-        hi_quantise(1, 0, 2)
+        q_quantise(1)
         gq(2)
+        hi_quantise(1, 0, 2)
+        rg(3)
         zmat(1)
+        hi_rows(1, 2, 2, psz, "z")
         s1(4)
         vmax(1)
-        hi_rows(1, 4, 1, psw, "w")
-        rg(3)
-        hi_quantise(1, 2, 2)
         gq(3)
         zmat(2)
-        s1(5)
+        hi_quantise(1, 2, 2)
+        hi_rows(1, 4, 1, psw, "w")
         vmax(2)
-        zmat(3)
+        s1(5)
         rg(4)
         hi_quantise(1, 4, 1)
         gq(4)
+        zmat(3)
         vmax(3)
+        rg(5)
         s1(6)
         zmat(4)
-        rg(5)
         vmax(4)
         gq(5)
-        subtract(0, 0)
-        s1(7)
         rg(6)
+        s1(7)
+        subtract(0, 0)
         subtract(0, 1)
         gq(6)
-        zmat(5)
         s1(8)
-        vmax(5)
+        exponent(0, 0)
         rg(7)
         subtract(0, 2)
+        subtract(0, 3)
         gq(7)
+        zmat(5)
+        vmax(5)
+        exponent(0, 1)
         zmat(6)
         s1(9)
         rg(8)
         vmax(6)
         gq(8)
-        subtract(0, 3)
-        zmat(7)
-
-        rg(9)
-        exponent(0, 0)
-        exponent(0, 1)
         exponent(0, 2)
         exponent(0, 3)
-        vmax(7)
-        gq(9)
+        zmat(7)
+        idle = psa.tile([P, H], F32, tag="a", name="idle_tail")
+        warm_up(idle, 256)
+
+        rg(9)
         subtract(0, 4)
+        gq(9)
+        vmax(7)
         product(0, 3)
         product(0, 0)
         product(0, 1)
@@ -416,6 +424,7 @@ def tile_haint_attention_kernel(tc, ht, ct, hi, W_as, W_ah, ba, v, W_a, out):
         open_sum(0, 0)
         add_to_sum(0, 0, 0)
         add_to_sum(0, 0, 1)
+        warm_up(idle, 256)
         zmat(8)
         vmax(8)
         zmat(9)
@@ -424,8 +433,8 @@ def tile_haint_attention_kernel(tc, ht, ct, hi, W_as, W_ah, ba, v, W_a, out):
         add_to_sum(0, 0, 3)
         add_to_sum(0, 0, 4)
         square_sum(0)
-        idle = psa.tile([P, H], F32, tag="a", name="idle_tail")
         warm_up(idle, 256)
+
         for t in range(T):
             subtract(1, t)
             exponent(1, t)
@@ -435,19 +444,15 @@ def tile_haint_attention_kernel(tc, ht, ct, hi, W_as, W_ah, ba, v, W_a, out):
         for n, t in enumerate((3, 0, 1, 2, 4)):
             add_to_sum(0, 1, t, n)
             add_to_sum(1, 0, n)
-            if n in (1, 4):
+            if n in (1, 3):
                 warm_up(idle, 256)
         for t in range(T):
             product(1, t)
         one_over(0)
         square_sum(1)
         one_over(1)
-        normalise(0)
-        store(0)
+        finish(0, ((0, 2),))
         open_sum(1, 1)
         for t in range(T):
             add_to_sum(1, 1, t)
-            if t in ():
-                warm_up(idle, 256)
-        normalise(1)
-        store(1)
+        finish(1, ((0, 1), (1, 2)))

@@ -21,8 +21,9 @@ A = 512
 
 PIN = True
 V_COLS = 352
-MUL_ON_G = ((0, 1, 2, 3), ())
-HALVED = ((1, 3), (1, 4))
+MUL_ON_G = ((0, 1, 2), ())
+HALVED = ((1, 2), (1, 3), (1, 4))
+SUB_HALVED = ((1, 0),)
 
 
 def tile_haint_attention_kernel(tc, ht, ct, hi, W_as, W_ah, ba, v, W_a, out):
@@ -31,8 +32,7 @@ def tile_haint_attention_kernel(tc, ht, ct, hi, W_as, W_ah, ba, v, W_a, out):
         if PIN:
             ctx.enter_context(tc.manual_schedule())
         keep = ctx.enter_context(tc.tile_pool(name="keep", bufs=1))
-        psa = ctx.enter_context(tc.psum_pool(name="psa", bufs=2))
-        psw = ctx.enter_context(tc.psum_pool(name="psw", bufs=1))
+        psa = ctx.enter_context(tc.psum_pool(name="psa", bufs=3))
         psz = ctx.enter_context(tc.psum_pool(name="psz", bufs=5))
 
         ident_f = keep.tile([P, P], F32)
@@ -206,6 +206,14 @@ def tile_haint_attention_kernel(tc, ht, ct, hi, W_as, W_ah, ba, v, W_a, out):
                         func=AF.Tanh, bias=ba_sb[:, j0 + jj : j0 + jj + 1], scale=1.0,
                     )
 
+        def g_regroup_pool(bt, t):
+            c0 = P * (T * bt + t)
+            nc.gpsimd.tensor_scalar(
+                out=gg[:, 4 * c0 : 4 * (c0 + P)].rearrange("p (c j) -> p c j", j=4),
+                in0=gt[:, :, c0 : c0 + P].rearrange("p j c -> p c j"),
+                scalar1=1.0, scalar2=0.0, op0=ALU.mult, op1=ALU.add,
+            )
+
         def g_regroup(bt, t0, count):
             c0 = P * (T * bt + t0)
             nc.vector.tensor_copy(
@@ -252,9 +260,12 @@ def tile_haint_attention_kernel(tc, ht, ct, hi, W_as, W_ah, ba, v, W_a, out):
                     )
 
         def subtract(bt, t):
-            nc.vector.tensor_tensor(
-                out=d[:, T * bt + t, :], in0=zs[(bt, t)][:], in1=m[:, bt, :], op=ALU.subtract
-            )
+            step = 256 if (bt, t) in SUB_HALVED else 512
+            for lo in range(0, 512, step):
+                nc.vector.tensor_tensor(
+                    out=d[:, T * bt + t, lo : lo + step], in0=zs[(bt, t)][:, lo : lo + step],
+                    in1=m[:, bt, lo : lo + step], op=ALU.subtract,
+                )
 
         def exponent(bt, t):
             nc.scalar.activation(out=e[:, T * bt + t, :], in_=d[:, T * bt + t, :], func=AF.Exp)
@@ -269,7 +280,7 @@ def tile_haint_attention_kernel(tc, ht, ct, hi, W_as, W_ah, ba, v, W_a, out):
             )
 
         def open_sum(bt, what):
-            pool, tag = ((psw, "w") if what == 0 else (psa, "a"), (psz, "z"))[bt]
+            pool, tag = ((psa, "a"), (psz, "z"))[bt]
             acc_t = pool.tile([P, 4, P], F32, tag=tag)
             sums[(bt, what)] = acc_t
 
@@ -315,7 +326,7 @@ def tile_haint_attention_kernel(tc, ht, ct, hi, W_as, W_ah, ba, v, W_a, out):
         w_regroup(1, 320)
         w_regroup(2, 320)
         w_quantise(1)
-        pb = psw.tile([P, P], BF16, tag="w")
+        pb = psa.tile([P, P], BF16, tag="a")
         nc.tensor.transpose(pb[:], ba16[:], ident_b[:])
         w_regroup(0, 320)
         w_quantise(2)
@@ -347,10 +358,13 @@ def tile_haint_attention_kernel(tc, ht, ct, hi, W_as, W_ah, ba, v, W_a, out):
         def gq(i, n=1):
             g_quantise(i // T, i % T, n)
 
+        def rgp(i):
+            g_regroup_pool(i // T, i % T)
+
         s1(0)
         wa_regroup()
-        w_quantise(3)
         hi_quantise(0, 3, 2)
+        w_quantise(3)
         rg(0)
         s1(1)
         s1(2)
@@ -369,12 +383,12 @@ def tile_haint_attention_kernel(tc, ht, ct, hi, W_as, W_ah, ba, v, W_a, out):
         rg(3)
         zmat(1)
         hi_rows(1, 2, 2, psz, "z")
+        hi_rows(1, 4, 1, psa, "a")
         s1(4)
         vmax(1)
         gq(3)
         zmat(2)
         hi_quantise(1, 2, 2)
-        hi_rows(1, 4, 1, psw, "w")
         vmax(2)
         s1(5)
         rg(4)
@@ -382,66 +396,63 @@ def tile_haint_attention_kernel(tc, ht, ct, hi, W_as, W_ah, ba, v, W_a, out):
         gq(4)
         zmat(3)
         vmax(3)
-        rg(5)
+        rgp(5)
         s1(6)
         zmat(4)
+        s1(7)
         vmax(4)
         gq(5)
-        rg(6)
-        s1(7)
+        rgp(6)
         subtract(0, 0)
         subtract(0, 1)
-        gq(6)
         s1(8)
-        exponent(0, 0)
-        rg(7)
         subtract(0, 2)
-        subtract(0, 3)
-        gq(7)
-        zmat(5)
-        vmax(5)
-        exponent(0, 1)
-        zmat(6)
+        rgp(7)
+        gq(6)
         s1(9)
-        rg(8)
-        vmax(6)
+        zmat(5)
+        subtract(0, 3)
+        rgp(8)
+        gq(7)
         gq(8)
-        exponent(0, 2)
-        exponent(0, 3)
+        zmat(6)
+        vmax(5)
+        subtract(0, 4)
+        rgp(9)
         zmat(7)
+        vmax(6)
+        exponent(0, 0)
+        gq(9)
+        zmat(8)
+        vmax(7)
+        exponent(0, 1)
+        exponent(0, 2)
         idle = psa.tile([P, H], F32, tag="a", name="idle_tail")
         warm_up(idle, 256)
-
-        rg(9)
-        subtract(0, 4)
-        gq(9)
-        vmax(7)
-        product(0, 3)
+        product(0, 2)
         product(0, 0)
         product(0, 1)
-        product(0, 2)
+        exponent(0, 3)
         exponent(0, 4)
         open_sum(0, 0)
         add_to_sum(0, 0, 0)
         add_to_sum(0, 0, 1)
-        warm_up(idle, 256)
-        zmat(8)
-        vmax(8)
         zmat(9)
+        vmax(8)
         vmax(9)
         add_to_sum(0, 0, 2)
         add_to_sum(0, 0, 3)
         add_to_sum(0, 0, 4)
         square_sum(0)
         warm_up(idle, 256)
-
         for t in range(T):
             subtract(1, t)
             exponent(1, t)
+        product(0, 3)
         product(0, 4)
         open_sum(0, 1)
         open_sum(1, 0)
-        for n, t in enumerate((3, 0, 1, 2, 4)):
+        for n, t in enumerate((2, 0, 1, 3, 4)):
             add_to_sum(0, 1, t, n)
             add_to_sum(1, 0, n)
             if n in (1, 3):

@@ -323,14 +323,14 @@ def tile_haint_attention_kernel(tc, ht, ct, hi, W_as, W_ah, ba, v, W_a, out):
         def warm_up(idle_bank, n):
             nc.tensor.matmul(out=idle_bank[:, 0:n], lhsT=ident_f[:], rhs=hi32[:, 0:n], start=True, stop=True)
 
-        w_regroup(1, 320)
-        w_regroup(2, 320)
+        w_regroup(1, 272)
+        w_regroup(2, 272)
         w_quantise(1)
         pb = psa.tile([P, P], BF16, tag="a")
         nc.tensor.transpose(pb[:], ba16[:], ident_b[:])
-        w_regroup(0, 320)
+        w_regroup(0, 272)
         w_quantise(2)
-        nc.vector.tensor_copy(out=ba_sb[:], in_=pb[:, 0:4])
+        nc.scalar.copy(out=ba_sb[:], in_=pb[:, 0:4])
         idle0 = psa.tile([P, H], F32, tag="a", name="idle_head")
         spin(idle0, 6)
         q_rows(0, psz, "z")
@@ -455,7 +455,7 @@ def tile_haint_attention_kernel(tc, ht, ct, hi, W_as, W_ah, ba, v, W_a, out):
         for n, t in enumerate((2, 0, 1, 3, 4)):
             add_to_sum(0, 1, t, n)
             add_to_sum(1, 0, n)
-            if n in (1, 3):
+            if n in (0, 2, 4):
                 warm_up(idle, 256)
         for t in range(T):
             product(1, t)

@@ -316,6 +316,11 @@ def tile_haint_attention_kernel(tc, ht, ct, hi, W_as, W_ah, ba, v, W_a, out):
                 )
                 nc.sync.dma_start(out=out[P * bt : P * (bt + 1), cols], in_=o_sb[:, bt, cols])
 
+        def spin_on(idle_bank, words):
+            nc.tensor.matmul(
+                out=idle_bank[:, 0:256], lhsT=ident_f[:], rhs=words.bitcast(F32)[:, 0:256], start=True, stop=True
+            )
+
         def spin(idle_bank, count):
             for k in range(count):
                 nc.tensor.matmul(out=idle_bank[:, 0:P], lhsT=ident_f[:], rhs=ident_f[:], start=True, stop=True)
@@ -323,24 +328,26 @@ def tile_haint_attention_kernel(tc, ht, ct, hi, W_as, W_ah, ba, v, W_a, out):
         def warm_up(idle_bank, n):
             nc.tensor.matmul(out=idle_bank[:, 0:n], lhsT=ident_f[:], rhs=hi32[:, 0:n], start=True, stop=True)
 
+        idle0 = psa.tile([P, H], F32, tag="a", name="idle_head")
         w_regroup(1, 272)
         w_regroup(2, 272)
         w_quantise(1)
-        pb = psa.tile([P, P], BF16, tag="a")
-        nc.tensor.transpose(pb[:], ba16[:], ident_b[:])
+        spin_on(idle0, raws[1])
+        spin_on(idle0, raws[2])
         w_regroup(0, 272)
         w_quantise(2)
-        nc.scalar.copy(out=ba_sb[:], in_=pb[:, 0:4])
-        idle0 = psa.tile([P, H], F32, tag="a", name="idle_head")
-        spin(idle0, 6)
+        spin_on(idle0, raws[0])
         q_rows(0, psz, "z")
         hi_rows(0, 0, 1, psz, "z")
-        spin(idle0, 3)
+        pb = psa.tile([P, P], BF16, tag="a")
+        nc.tensor.transpose(pb[:], ba16[:], ident_b[:])
+        spin(idle0, 2)
         w_quantise(0)
         q_quantise(0)
         hi_quantise(0, 0, 1)
         hi_rows(0, 1, 2, psz, "z")
         hi_rows(0, 3, 2, psz, "z")
+        nc.scalar.copy(out=ba_sb[:], in_=pb[:, 0:4])
         hi_quantise(0, 1, 2)
 
         def zmat(i):

@@ -21,7 +21,7 @@ A = 512
 
 PIN = True
 V_COLS = 352
-MUL_ON_G = ((0, 1, 2), ())
+MUL_ON_G = ((0, 1, 2, 3, 4), ())
 HALVED = ((1, 2), (1, 3), (1, 4))
 SUB_HALVED = ((1, 0),)
 
@@ -237,6 +237,7 @@ def tile_haint_attention_kernel(tc, ht, ct, hi, W_as, W_ah, ba, v, W_a, out):
         o_sb = keep.tile([P, NBT, H], F32)
         zs = {}
         sums = {}
+        his = {}
 
         def stage2(bt, t):
             z = psz.tile([P, H], F32, tag="z")
@@ -279,6 +280,23 @@ def tile_haint_attention_kernel(tc, ht, ct, hi, W_as, W_ah, ba, v, W_a, out):
                 in1=hi_grp[:, H * k : H * (k + 1)].rearrange("p (b j) -> p j b", j=4), op=ALU.mult,
             )
 
+        def hi_again(bt, t0, count, pool, tag):
+            xt = pool.tile([P, 4, P], F32, tag=tag)
+            for i in range(2 * count):
+                nc.tensor.transpose(
+                    xt[:, i, :], hi32[:, 256 * (T * bt + t0) + P * i : 256 * (T * bt + t0) + P * (i + 1)], ident_f[:]
+                )
+            for tt in range(count):
+                his[(bt, t0 + tt)] = xt[:].rearrange("p c b -> p (c b)").bitcast(BF16)[:, 512 * tt : 512 * (tt + 1)]
+
+        def product_ps(bt, t):
+            k = T * bt + t
+            nc.vector.tensor_tensor(
+                out=w[:, k, :].rearrange("p (u e b) -> p u e b", u=2, e=2),
+                in0=e[:, k, :].rearrange("p (u e b) -> p u e b", u=2, e=2),
+                in1=his[(bt, t)].rearrange("p (u b e) -> p u e b", u=2, e=2), op=ALU.mult,
+            )
+
         def open_sum(bt, what):
             pool, tag = ((psa, "a"), (psz, "z"))[bt]
             acc_t = pool.tile([P, 4, P], F32, tag=tag)
@@ -305,6 +323,25 @@ def tile_haint_attention_kernel(tc, ht, ct, hi, W_as, W_ah, ba, v, W_a, out):
 
         def one_over(bt):
             nc.scalar.activation(out=r[:, bt, :], in_=s2[:, bt, :], func=AF.Abs_reciprocal_sqrt)
+
+        def one_over_root(bt):
+            nc.scalar.activation(
+                out=r[:, bt, :].rearrange("p (u q e) -> p u q e", u=2, e=2),
+                in_=natural(sums[(bt, 0)][:]), func=AF.Abs_reciprocal_sqrt,
+            )
+
+        def finish_twice(bt):
+            for u in range(2):
+                cols = slice(256 * u, 256 * (u + 1))
+                nc.vector.tensor_tensor(
+                    out=s2[:, bt, cols].rearrange("p (u q e) -> p u q e", e=2, q=P),
+                    in0=natural(sums[(bt, 1)][:])[:, u : u + 1, :, :],
+                    in1=r[:, bt, cols].rearrange("p (u q e) -> p u q e", e=2, q=P), op=ALU.mult,
+                )
+            for u in range(2):
+                cols = slice(256 * u, 256 * (u + 1))
+                nc.vector.tensor_tensor(out=o_sb[:, bt, cols], in0=s2[:, bt, cols], in1=r[:, bt, cols], op=ALU.mult)
+                nc.sync.dma_start(out=out[P * bt : P * (bt + 1), cols], in_=o_sb[:, bt, cols])
 
         def finish(bt, halves):
             for u0, u1 in halves:
@@ -434,13 +471,16 @@ def tile_haint_attention_kernel(tc, ht, ct, hi, W_as, W_ah, ba, v, W_a, out):
         vmax(7)
         exponent(0, 1)
         exponent(0, 2)
-        idle = psa.tile([P, H], F32, tag="a", name="idle_tail")
+        open_sum(0, 1)
+        idle = sums[(0, 1)][:].rearrange("p c b -> p (c b)")
         warm_up(idle, 256)
         product(0, 2)
         product(0, 0)
         product(0, 1)
         exponent(0, 3)
+        product(0, 3)
         exponent(0, 4)
+        product(0, 4)
         open_sum(0, 0)
         add_to_sum(0, 0, 0)
         add_to_sum(0, 0, 1)
@@ -451,26 +491,35 @@ def tile_haint_attention_kernel(tc, ht, ct, hi, W_as, W_ah, ba, v, W_a, out):
         add_to_sum(0, 0, 3)
         add_to_sum(0, 0, 4)
         square_sum(0)
+        hi_again(1, 0, 2, psa, "a")
         warm_up(idle, 256)
+        idle2 = sums[(0, 0)][:].rearrange("p c b -> p (c b)")
         for t in range(T):
             subtract(1, t)
             exponent(1, t)
-        product(0, 3)
-        product(0, 4)
-        open_sum(0, 1)
+        add_to_sum(0, 1, 2, 0)
         open_sum(1, 0)
-        for n, t in enumerate((2, 0, 1, 3, 4)):
-            add_to_sum(0, 1, t, n)
-            add_to_sum(1, 0, n)
-            if n in (0, 2, 4):
-                warm_up(idle, 256)
+        add_to_sum(0, 1, 0, 1)
+        add_to_sum(1, 0, 0)
+        hi_again(1, 2, 2, psz, "z")
+        add_to_sum(1, 0, 1)
+        hi_again(1, 4, 1, psz, "z")
+        warm_up(idle2, 256)
+        add_to_sum(0, 1, 1, 2)
+        add_to_sum(1, 0, 2)
+        add_to_sum(1, 0, 3)
+        add_to_sum(1, 0, 4)
         for t in range(T):
-            product(1, t)
+            product_ps(1, t)
+        open_sum(1, 1)
+        add_to_sum(0, 1, 3, 3)
+        for t in range(3):
+            add_to_sum(1, 1, t)
+        add_to_sum(0, 1, 4, 4)
+        for t in range(3, T):
+            add_to_sum(1, 1, t)
         one_over(0)
         square_sum(1)
         one_over(1)
         finish(0, ((0, 2),))
-        open_sum(1, 1)
-        for t in range(T):
-            add_to_sum(1, 1, t)
         finish(1, ((0, 1), (1, 2)))

from contextlib import ExitStack

import concourse.mybir as mybir
from concourse.masks import make_identity

FLOPS = 2 * (256 * 1024 * 512 + 2 * 1280 * 512 * 512)

FP8X4 = mybir.dt.float8_e4m3fn_x4
BF16 = mybir.dt.bfloat16
F32 = mybir.dt.float32
U32 = mybir.dt.uint32
U8 = mybir.dt.uint8
AF = mybir.ActivationFunctionType
ALU = mybir.AluOpType

P = 128
NBT = 2
T = 5
H = 512
A = 512

PIN = True
V_COLS = 352
MUL_ON_G = ((0, 1, 2, 3, 4), ())
HALVED = ((1, 2), (1, 3), (1, 4))
SUB_HALVED = ((1, 0),)


def tile_haint_attention_kernel(tc, ht, ct, hi, W_as, W_ah, ba, v, W_a, out):
    nc = tc.nc
    with ExitStack() as ctx:
        if PIN:
            ctx.enter_context(tc.manual_schedule())
        keep = ctx.enter_context(tc.tile_pool(name="keep", bufs=1))
        psa = ctx.enter_context(tc.psum_pool(name="psa", bufs=3))
        psz = ctx.enter_context(tc.psum_pool(name="psz", bufs=5))

        ident_f = keep.tile([P, P], F32)
        make_identity(nc, ident_f[:])
        ident_b = keep.tile([P, P], BF16)
        make_identity(nc, ident_b[:])
        ba16 = keep.tile([P, P], BF16)
        nc.vector.memset(ba16[:], 0.0)

        wah_raw = keep.tile([P, 4 * A], BF16)
        was_raw = keep.tile([P, 2 * 4 * A], BF16)
        wa_raw = keep.tile([P, 4 * H], BF16)
        q_sb = keep.tile([P, NBT * 2 * H], BF16)
        hi_sb = keep.tile([P, NBT * T * H], BF16)

        def load_k_pairs(dst, rows):
            nc.sync.dma_start(
                out=dst.rearrange("p (u x) -> p u x", u=2),
                in_=rows.rearrange("(u q e) a -> q u (e a)", u=2, e=2),
            )

        def load_q(bt):
            nc.sync.dma_start(out=q_sb[:, 2 * H * bt : 2 * H * bt + H], in_=ht[P * bt : P * (bt + 1), :])
            nc.sync.dma_start(out=q_sb[:, 2 * H * bt + H : 2 * H * (bt + 1)], in_=ct[P * bt : P * (bt + 1), :])

        def load_hi(bt, t0, t1):
            nc.sync.dma_start(
                out=hi_sb[:, H * (T * bt + t0) : H * (T * bt + t1)],
                in_=hi[P * bt : P * (bt + 1), t0:t1, :].rearrange("b t h -> b (t h)"),
            )

        nc.scalar.dma_start(out=ba16[0:4, :], in_=ba.rearrange("o (j p) -> (o j) p", p=P))
        load_k_pairs(was_raw[:, 0 : 4 * A], W_as[0:512, :])
        load_k_pairs(was_raw[:, 4 * A : 8 * A], W_as[512:1024, :])
        load_k_pairs(wah_raw[:], W_ah)
        load_q(0)
        load_hi(0, 0, 1)
        load_hi(0, 1, 5)
        nc.sync.dma_start(
            out=wa_raw[:].rearrange("p (t n) -> p t n", t=4),
            in_=W_a.rearrange("(t p) n -> p t n", p=P),
        )
        load_q(1)
        load_hi(1, 0, 5)

        w_codes = keep.tile([P, 4 * 512], U32, align_bytes=64)
        w_scales = keep.tile([P, 4 * 512], U8, align_bytes=64)
        w_grp = keep.tile([P, 4 * 2048], BF16, align_bytes=64)
        raws = [wah_raw[:], was_raw[:, 0:2048], was_raw[:, 2048:4096], wa_raw[:]]

        def quantise(codes, scales, src):
            nc.vector.quantize_mx(out=codes.bitcast(FP8X4), scales=scales, in_=src)

        def w_regroup(i, v_cols, s_end=512):
            src = raws[i].rearrange("p (t c) -> p t c", t=4)
            for copy, lo, hi_c in ((nc.vector.tensor_copy, 0, v_cols), (nc.scalar.copy, v_cols, s_end)):
                if hi_c > lo:
                    copy(
                        out=w_grp[:, 2048 * i + 4 * lo : 2048 * i + 4 * hi_c].rearrange(
                            "p (c i t) -> p c t i", i=4, t=4
                        ),
                        in_=src[:, :, lo:hi_c].rearrange("p t (c i) -> p c t i", i=4),
                    )

        def w_identity(i, lo, cols):
            ps = psa.tile([P, 4, cols], BF16, tag="a")
            for t in range(4):
                nc.tensor.matmul(
                    out=ps[:, t, :], lhsT=ident_b[:], rhs=raws[i][:, 512 * t + lo : 512 * t + lo + cols],
                    start=True, stop=True,
                )
            nc.scalar.copy(
                out=w_grp[:, 2048 * i + 4 * lo : 2048 * i + 4 * (lo + cols)].rearrange("p (c t) -> p c t", t=4),
                in_=ps[:].rearrange("p t c -> p c t"),
            )

        def wa_regroup():
            src = raws[3].rearrange("p (t u q i e) -> p u e q t i", t=4, u=2, i=4, e=2)
            for u in range(2):
                copy = nc.vector.tensor_copy
                for ee in range(2):
                    lo = 2048 * 3 + 512 * (2 * u + ee)
                    copy(
                        out=w_grp[:, lo : lo + 512].rearrange("p (q i t) -> p q t i", i=4, t=4),
                        in_=src[:, u, ee, :, :, :],
                    )

        def w_quantise(i):
            quantise(
                w_codes[:, 512 * i : 512 * (i + 1)],
                w_scales[:, 512 * i : 512 * (i + 1)],
                w_grp[:, 2048 * i : 2048 * (i + 1)],
            )

        q32 = q_sb[:].bitcast(F32)
        hi32 = hi_sb[:].bitcast(F32)
        q_codes = keep.tile([P, NBT * 2 * P], U32, align_bytes=64)
        q_scales = keep.tile([P, NBT * 2 * P], U8, align_bytes=64)
        hi_codes = keep.tile([P, NBT * T * P], U32, align_bytes=64)
        hi_scales = keep.tile([P, NBT * T * P], U8, align_bytes=64)
        q_grp = keep.tile([P, NBT * 2 * P * 4], BF16, align_bytes=64)
        hi_grp = keep.tile([P, NBT * T * P * 4], BF16, align_bytes=64)
        q_grp32 = q_grp[:].bitcast(F32)
        hi_grp32 = hi_grp[:].bitcast(F32)

        def transpose_words(pool, tag, src32, dst32, first, count):
            xt = pool.tile([P, 4, P], F32, tag=tag)
            for i in range(2 * count):
                nc.tensor.transpose(
                    xt[:, i, :], src32[:, 256 * first + P * i : 256 * first + P * (i + 1)], ident_f[:]
                )
            nc.scalar.copy(
                out=dst32[:, 256 * first : 256 * (first + count)].rearrange(
                    "p (g b u) -> p g b u", g=count, u=2
                ),
                in_=xt[:, 0 : 2 * count, :].rearrange("p (g u) b -> p g b u", u=2),
            )

        def q_rows(bt, pool, tag):
            transpose_words(pool, tag, q32, q_grp32, 2 * bt, 2)

        def q_quantise(bt):
            quantise(
                q_codes[:, 256 * bt : 256 * (bt + 1)], q_scales[:, 256 * bt : 256 * (bt + 1)],
                q_grp[:, 1024 * bt : 1024 * (bt + 1)],
            )

        def hi_rows(bt, t0, count, pool, tag):
            transpose_words(pool, tag, hi32, hi_grp32, T * bt + t0, count)

        def hi_quantise(bt, t0, count):
            c0 = P * (T * bt + t0)
            quantise(
                hi_codes[:, c0 : c0 + P * count], hi_scales[:, c0 : c0 + P * count],
                hi_grp[:, 4 * c0 : 4 * (c0 + P * count)],
            )

        g_codes = keep.tile([P, NBT * T * P], U32, align_bytes=64)
        g_scales = keep.tile([P, NBT * T * P], U8, align_bytes=64)
        gt = keep.tile([P, 4, NBT * T * P], BF16)
        gg = keep.tile([P, NBT * T * P * 4], BF16, align_bytes=64)
        ba_sb = keep.tile([P, 4], F32)

        def mx(out_ap, l_codes, l_scales, lc, r_codes, r_scales, rc, n, start, stop):
            nc.tensor.matmul_mx(
                out=out_ap,
                lhsT=l_codes[:, lc : lc + P].bitcast(FP8X4),
                lhsT_scale=l_scales[:, lc : lc + P],
                rhs=r_codes[:, rc : rc + n].bitcast(FP8X4),
                rhs_scale=r_scales[:, rc : rc + n],
                start=start,
                stop=stop,
            )

        def stage1_group(o, bt, j, t):
            mx(o, w_codes, w_scales, P * j, hi_codes, hi_scales, P * (T * bt + t), P, True, False)
            mx(o, w_codes, w_scales, 512 + P * j, q_codes, q_scales, P * (2 * bt), P, False, False)
            mx(o, w_codes, w_scales, 1024 + P * j, q_codes, q_scales, P * (2 * bt + 1), P, False, True)

        def stage1(bt, t0, count):
            c0 = P * (T * bt + t0)
            j_per_bank = 4 // count
            for j0 in range(0, 4, j_per_bank):
                acc = psa.tile([P, j_per_bank, count * P], F32, tag="a")
                for jj in range(j_per_bank):
                    for tt in range(count):
                        stage1_group(acc[:, jj, P * tt : P * (tt + 1)], bt, j0 + jj, t0 + tt)
                for jj in range(j_per_bank):
                    nc.scalar.activation(
                        out=gt[:, j0 + jj, c0 : c0 + P * count], in_=acc[:, jj, :],
                        func=AF.Tanh, bias=ba_sb[:, j0 + jj : j0 + jj + 1], scale=1.0,
                    )

        def g_regroup_pool(bt, t):
            c0 = P * (T * bt + t)
            nc.gpsimd.tensor_scalar(
                out=gg[:, 4 * c0 : 4 * (c0 + P)].rearrange("p (c j) -> p c j", j=4),
                in0=gt[:, :, c0 : c0 + P].rearrange("p j c -> p c j"),
                scalar1=1.0, scalar2=0.0, op0=ALU.mult, op1=ALU.add,
            )

        def g_regroup(bt, t0, count):
            c0 = P * (T * bt + t0)
            nc.vector.tensor_copy(
                out=gg[:, 4 * c0 : 4 * (c0 + P * count)].rearrange("p (c i j) -> p c j i", i=4, j=4),
                in_=gt[:, :, c0 : c0 + P * count].rearrange("p j (c i) -> p c j i", i=4),
            )

        def g_quantise(bt, t0, count):
            c0 = P * (T * bt + t0)
            quantise(
                g_codes[:, c0 : c0 + P * count], g_scales[:, c0 : c0 + P * count],
                gg[:, 4 * c0 : 4 * (c0 + P * count)],
            )

        m = keep.tile([P, NBT, H], F32)
        d = keep.tile([P, NBT * T, H], F32)
        e = keep.tile([P, NBT * T, H], F32)
        w = keep.tile([P, NBT * T, H], F32)
        s2 = keep.tile([P, NBT, H], F32)
        r = keep.tile([P, NBT, H], F32)
        o_sb = keep.tile([P, NBT, H], F32)
        zs = {}
        sums = {}
        his = {}

        def stage2(bt, t):
            z = psz.tile([P, H], F32, tag="z")
            for j in range(4):
                mx(
                    z[:, P * j : P * (j + 1)], w_codes, w_scales, 1536 + P * j,
                    g_codes, g_scales, P * (T * bt + t), P, True, True,
                )
            zs[(bt, t)] = z

        def maximum(bt, t):
            z = zs[(bt, t)]
            if t == 0:
                nc.scalar.copy(out=m[:, bt, :], in_=z[:])
            else:
                step = 256 if (bt, t) in HALVED else 512
                for lo in range(0, 512, step):
                    nc.vector.tensor_tensor(
                        out=m[:, bt, lo : lo + step], in0=z[:, lo : lo + step], in1=m[:, bt, lo : lo + step],
                        op=ALU.max,
                    )

        def subtract(bt, t):
            step = 256 if (bt, t) in SUB_HALVED else 512
            for lo in range(0, 512, step):
                nc.vector.tensor_tensor(
                    out=d[:, T * bt + t, lo : lo + step], in0=zs[(bt, t)][:, lo : lo + step],
                    in1=m[:, bt, lo : lo + step], op=ALU.subtract,
                )

        def exponent(bt, t):
            nc.scalar.activation(out=e[:, T * bt + t, :], in_=d[:, T * bt + t, :], func=AF.Exp)

        def product(bt, t):
            k = T * bt + t
            eng = nc.gpsimd if t in MUL_ON_G[bt] else nc.vector
            eng.tensor_tensor(
                out=w[:, k, :].rearrange("p (j b) -> p j b", j=4),
                in0=e[:, k, :].rearrange("p (j b) -> p j b", j=4),
                in1=hi_grp[:, H * k : H * (k + 1)].rearrange("p (b j) -> p j b", j=4), op=ALU.mult,
            )

        def hi_again(bt, t0, count, pool, tag):
            xt = pool.tile([P, 4, P], F32, tag=tag)
            for i in range(2 * count):
                nc.tensor.transpose(
                    xt[:, i, :], hi32[:, 256 * (T * bt + t0) + P * i : 256 * (T * bt + t0) + P * (i + 1)], ident_f[:]
                )
            for tt in range(count):
                his[(bt, t0 + tt)] = xt[:].rearrange("p c b -> p (c b)").bitcast(BF16)[:, 512 * tt : 512 * (tt + 1)]

        def product_ps(bt, t):
            k = T * bt + t
            nc.vector.tensor_tensor(
                out=w[:, k, :].rearrange("p (u e b) -> p u e b", u=2, e=2),
                in0=e[:, k, :].rearrange("p (u e b) -> p u e b", u=2, e=2),
                in1=his[(bt, t)].rearrange("p (u b e) -> p u e b", u=2, e=2), op=ALU.mult,
            )

        def open_sum(bt, what):
            pool, tag = ((psa, "a"), (psz, "z"))[bt]
            acc_t = pool.tile([P, 4, P], F32, tag=tag)
            sums[(bt, what)] = acc_t

        def add_to_sum(bt, what, t, place=None):
            place = t if place is None else place
            src = (e, w)[what]
            for c in range(4):
                nc.tensor.matmul(
                    out=sums[(bt, what)][:, c, :], lhsT=src[:, T * bt + t, P * c : P * (c + 1)],
                    rhs=ident_f[:], is_transpose=True,
                    start=(place == 0 and c == 0), stop=(place == T - 1 and c == 3),
                )

        def natural(ap):
            return ap.rearrange("p (u e) q -> p u q e", u=2)

        def square_sum(bt):
            nc.scalar.activation(
                out=s2[:, bt, :].rearrange("p (u q e) -> p u q e", u=2, e=2),
                in_=natural(sums[(bt, 0)][:]), func=AF.Square,
            )

        def one_over(bt):
            nc.scalar.activation(out=r[:, bt, :], in_=s2[:, bt, :], func=AF.Abs_reciprocal_sqrt)

        def one_over_root(bt):
            nc.scalar.activation(
                out=r[:, bt, :].rearrange("p (u q e) -> p u q e", u=2, e=2),
                in_=natural(sums[(bt, 0)][:]), func=AF.Abs_reciprocal_sqrt,
            )

        def finish_twice(bt):
            for u in range(2):
                cols = slice(256 * u, 256 * (u + 1))
                nc.vector.tensor_tensor(
                    out=s2[:, bt, cols].rearrange("p (u q e) -> p u q e", e=2, q=P),
                    in0=natural(sums[(bt, 1)][:])[:, u : u + 1, :, :],
                    in1=r[:, bt, cols].rearrange("p (u q e) -> p u q e", e=2, q=P), op=ALU.mult,
                )
            for u in range(2):
                cols = slice(256 * u, 256 * (u + 1))
                nc.vector.tensor_tensor(out=o_sb[:, bt, cols], in0=s2[:, bt, cols], in1=r[:, bt, cols], op=ALU.mult)
                nc.sync.dma_start(out=out[P * bt : P * (bt + 1), cols], in_=o_sb[:, bt, cols])

        def finish(bt, halves):
            for u0, u1 in halves:
                cols = slice(256 * u0, 256 * u1)
                nc.vector.tensor_tensor(
                    out=o_sb[:, bt, cols].rearrange("p (u q e) -> p u q e", e=2, q=P),
                    in0=natural(sums[(bt, 1)][:])[:, u0:u1, :, :],
                    in1=r[:, bt, cols].rearrange("p (u q e) -> p u q e", e=2, q=P), op=ALU.mult,
                )
                nc.sync.dma_start(out=out[P * bt : P * (bt + 1), cols], in_=o_sb[:, bt, cols])

        def spin_on(idle_bank, words):
            nc.tensor.matmul(
                out=idle_bank[:, 0:256], lhsT=ident_f[:], rhs=words.bitcast(F32)[:, 0:256], start=True, stop=True
            )

        def spin(idle_bank, count):
            for k in range(count):
                nc.tensor.matmul(out=idle_bank[:, 0:P], lhsT=ident_f[:], rhs=ident_f[:], start=True, stop=True)

        def warm_up(idle_bank, n):
            nc.tensor.matmul(out=idle_bank[:, 0:n], lhsT=ident_f[:], rhs=hi32[:, 0:n], start=True, stop=True)

        idle0 = psa.tile([P, H], F32, tag="a", name="idle_head")
        w_regroup(1, 272)
        w_regroup(2, 272)
        w_quantise(1)
        spin_on(idle0, raws[1])
        spin_on(idle0, raws[2])
        w_regroup(0, 272)
        w_quantise(2)
        spin_on(idle0, raws[0])
        q_rows(0, psz, "z")
        hi_rows(0, 0, 1, psz, "z")
        pb = psa.tile([P, P], BF16, tag="a")
        nc.tensor.transpose(pb[:], ba16[:], ident_b[:])
        spin(idle0, 2)
        w_quantise(0)
        q_quantise(0)
        hi_quantise(0, 0, 1)
        hi_rows(0, 1, 2, psz, "z")
        hi_rows(0, 3, 2, psz, "z")
        nc.scalar.copy(out=ba_sb[:], in_=pb[:, 0:4])
        hi_quantise(0, 1, 2)

        def zmat(i):
            stage2(i // T, i % T)

        def vmax(i):
            maximum(i // T, i % T)

        def s1(i, n=1):
            stage1(i // T, i % T, n)

        def rg(i, n=1):
            g_regroup(i // T, i % T, n)

        def gq(i, n=1):
            g_quantise(i // T, i % T, n)

        def rgp(i):
            g_regroup_pool(i // T, i % T)

        s1(0)
        wa_regroup()
        hi_quantise(0, 3, 2)
        w_quantise(3)
        rg(0)
        s1(1)
        s1(2)
        rg(1)
        gq(0)
        gq(1)
        q_rows(1, psz, "z")
        hi_rows(1, 0, 2, psz, "z")
        rg(2)
        s1(3)
        zmat(0)
        vmax(0)
        q_quantise(1)
        gq(2)
        hi_quantise(1, 0, 2)
        rg(3)
        zmat(1)
        hi_rows(1, 2, 2, psz, "z")
        hi_rows(1, 4, 1, psa, "a")
        s1(4)
        vmax(1)
        gq(3)
        zmat(2)
        hi_quantise(1, 2, 2)
        vmax(2)
        s1(5)
        rg(4)
        hi_quantise(1, 4, 1)
        gq(4)
        zmat(3)
        vmax(3)
        rgp(5)
        s1(6)
        zmat(4)
        s1(7)
        vmax(4)
        gq(5)
        rgp(6)
        subtract(0, 0)
        subtract(0, 1)
        s1(8)
        subtract(0, 2)
        rgp(7)
        gq(6)
        s1(9)
        zmat(5)
        subtract(0, 3)
        rgp(8)
        gq(7)
        gq(8)
        zmat(6)
        vmax(5)
        subtract(0, 4)
        rgp(9)
        zmat(7)
        vmax(6)
        exponent(0, 0)
        gq(9)
        zmat(8)
        vmax(7)
        exponent(0, 1)
        exponent(0, 2)
        open_sum(0, 1)
        idle = sums[(0, 1)][:].rearrange("p c b -> p (c b)")
        warm_up(idle, 256)
        product(0, 2)
        product(0, 0)
        product(0, 1)
        exponent(0, 3)
        product(0, 3)
        exponent(0, 4)
        product(0, 4)
        open_sum(0, 0)
        add_to_sum(0, 0, 0)
        add_to_sum(0, 0, 1)
        zmat(9)
        vmax(8)
        vmax(9)
        add_to_sum(0, 0, 2)
        add_to_sum(0, 0, 3)
        add_to_sum(0, 0, 4)
        square_sum(0)
        hi_again(1, 0, 2, psa, "a")
        warm_up(idle, 256)
        idle2 = sums[(0, 0)][:].rearrange("p c b -> p (c b)")
        for t in range(T):
            subtract(1, t)
            exponent(1, t)
        add_to_sum(0, 1, 2, 0)
        open_sum(1, 0)
        add_to_sum(0, 1, 0, 1)
        add_to_sum(1, 0, 0)
        hi_again(1, 2, 2, psz, "z")
        add_to_sum(1, 0, 1)
        hi_again(1, 4, 1, psz, "z")
        warm_up(idle2, 256)
        add_to_sum(0, 1, 1, 2)
        add_to_sum(1, 0, 2)
        add_to_sum(1, 0, 3)
        add_to_sum(1, 0, 4)
        for t in range(T):
            product_ps(1, t)
        open_sum(1, 1)
        add_to_sum(0, 1, 3, 3)
        for t in range(3):
            add_to_sum(1, 1, t)
        add_to_sum(0, 1, 4, 4)
        for t in range(3, T):
            add_to_sum(1, 1, t)
        one_over(0)
        square_sum(1)
        one_over(1)
        finish(0, ((0, 2),))
        finish(1, ((0, 1), (1, 2)))
